import numpy as np
import ml_dtypes


def mxq(x, axis, fmt="e4m3"):
    dtype, down = {"e4m3": (ml_dtypes.float8_e4m3fn, 7), "e5m2": (ml_dtypes.float8_e5m2, 14)}[fmt]
    v = np.moveaxis(np.asarray(x, np.float32).astype(ml_dtypes.bfloat16).astype(np.float64), axis, -1)
    blocks = v.reshape(v.shape[:-1] + (-1, 32))
    amax = np.abs(blocks).max(-1, keepdims=True)
    byte = np.maximum(np.where(amax > 0, np.frexp(amax)[1] - 1 + 127, 0) - down, 1)
    scale = np.exp2(byte - 127.0)
    codes = (blocks / scale).astype(np.float32).astype(dtype).astype(np.float64)
    return np.moveaxis((codes * scale).reshape(v.shape), -1, axis)


WIDE = False


def mx_kscale(k):
    if not WIDE:
        return np.ones(k)
    levels = np.array([10, -10, 5, -5, 0])
    a = np.random.permutation(np.resize(levels, k // 512 * 4)).reshape(k // 512, 4)
    idx = np.arange(k)
    return np.exp2(a[idx // 512, idx % 128 // 32])


BF16 = ml_dtypes.bfloat16


def bf(x):
    return np.asarray(x, np.float32).astype(BF16)


def f64(x):
    return np.asarray(x).astype(np.float64)


E2M1 = np.array([0.0, 0.5, 1.0, 1.5, 2.0, 3.0, 4.0, 6.0, -0.0, -0.5, -1.0, -1.5, -2.0, -3.0, -4.0, -6.0])


def pack_weight(w, fmt):
    k, n = w.shape
    w = f64(bf(w)).reshape(k // 32, 32, n)
    amax = np.abs(w).max(1)
    if fmt == "e4m3":
        byte = np.frexp(amax)[1] - 1 + 127 - 7
    else:
        mant, ex = np.frexp(amax / 6.0)
        byte = np.where(mant > 0.5, ex, ex - 1) + 127
    byte = np.clip(np.where(amax > 0, byte, 1), 1, 254)
    scaled = (w * np.exp2(127.0 - byte)[:, None, :]).reshape(k, n).astype(np.float32)
    by_word = np.ascontiguousarray(scaled.reshape(k // 512, 128, 4, n).transpose(0, 1, 3, 2))
    if fmt == "e4m3":
        words = by_word.astype(ml_dtypes.float8_e4m3fn).view(np.uint8)
    else:
        c = by_word.astype(ml_dtypes.float4_e2m1fn).view(np.uint8) & 0xF
        words = c[..., 0::2] | (c[..., 1::2] << 4)
    return np.ascontiguousarray(words), np.ascontiguousarray(byte.astype(np.uint8).reshape(k // 512, 16, n))


def unpack_weight(words, scales, fmt):
    g, p, n, _ = words.shape
    if fmt == "e4m3":
        vals = np.ascontiguousarray(words).view(ml_dtypes.float8_e4m3fn).astype(np.float64)
    else:
        nib = np.empty((g, p, n, 4), np.uint8)
        nib[..., 0::2] = words & 0xF
        nib[..., 1::2] = words >> 4
        vals = E2M1[nib]
    vals = vals * np.repeat(np.exp2(scales.astype(np.float64) - 127.0), 8, axis=1)[..., None]
    return vals.transpose(0, 1, 3, 2).reshape(g * 512, n)


E, T, H, F = 4, 256, 512, 2048


def silu(v):
    return v / (1.0 + np.exp(-v))


def setup_inputs():
    s, t = mx_kscale(H), mx_kscale(F)
    hidden_states = bf(np.random.standard_normal((E * T, H)) * s)
    gate_stack = np.random.standard_normal((E, H, F)) * (1.0 / np.sqrt(H)) / s[:, None]
    up_stack = np.random.standard_normal((E, H, F)) * (1.0 / np.sqrt(H)) / s[:, None] * t
    down_stack = np.random.standard_normal((E, F, H)) * (1.5 / np.sqrt(F)) / t[:, None]
    gate_words, gate_scales = pack_weight(gate_stack.reshape(-1, F), "e4m3")
    up_words, up_scales = pack_weight(up_stack.reshape(-1, F), "e4m3")
    down_words, down_scales = pack_weight(down_stack.reshape(-1, H), "e4m3")
    return {"hidden_states": hidden_states,
            "gate_w_words": gate_words, "gate_w_scales": gate_scales,
            "up_w_words": up_words, "up_w_scales": up_scales,
            "down_w_words": down_words, "down_w_scales": down_scales}


def reference(hidden_states, gate_w_words, gate_w_scales, up_w_words, up_w_scales, down_w_words, down_w_scales):
    x = f64(hidden_states).reshape(E, -1, H)
    xq = mxq(x, 2, "e4m3")
    gate = xq @ unpack_weight(gate_w_words, gate_w_scales, "e4m3").reshape(E, H, F)
    up = xq @ unpack_weight(up_w_words, up_w_scales, "e4m3").reshape(E, H, F)
    h = up * silu(gate)
    out = mxq(h, 2, "e4m3") @ unpack_weight(down_w_words, down_w_scales, "e4m3").reshape(E, F, H)
    return out.reshape(-1, H)

@@ -1,0 +1,221 @@
+from contextlib import ExitStack
+
+import concourse.mybir as mybir
+from concourse.masks import make_identity
+
+F32 = mybir.dt.float32
+BF16 = mybir.dt.bfloat16
+I32 = mybir.dt.int32
+U32 = mybir.dt.uint32
+U8 = mybir.dt.uint8
+FP8X4 = mybir.dt.float8_e4m3fn_x4
+SILU = mybir.ActivationFunctionType.Silu
+MULT = mybir.AluOpType.mult
+
+P = 128
+PACK = 4
+K_PASS = P * PACK
+EXPERTS, TOKENS, HIDDEN, WIDE = 4, 256, 512, 2048
+TOKEN_TILES = TOKENS // P
+CHUNKS = WIDE // K_PASS
+QUADRANTS = 4
+FIRST_PIECES = 4
+
+FLOPS = 3 * 2 * EXPERTS * TOKENS * HIDDEN * WIDE
+
+
+def tile_llama4textexperts_e_kernel(
+    tc,
+    hidden_states,
+    gate_w_words,
+    gate_w_scales,
+    up_w_words,
+    up_w_scales,
+    down_w_words,
+    down_w_scales,
+    out,
+):
+    nc = tc.nc
+    with ExitStack() as stack:
+        keep = stack.enter_context(tc.tile_pool(name="keep", bufs=1))
+        work = stack.enter_context(tc.tile_pool(name="work", bufs=3))
+        psum = stack.enter_context(tc.psum_pool(name="psum", bufs=2))
+
+        x_sb = keep.tile([P, EXPERTS, TOKEN_TILES, HIDDEN], BF16)
+        x_grouped = keep.tile([P, EXPERTS, TOKENS, PACK], BF16, align_bytes=64)
+        x_codes = keep.tile([P, EXPERTS, TOKENS], U32, align_bytes=64)
+        x_scales = keep.tile([P, EXPERTS, TOKENS], U8, align_bytes=64)
+        gate_words = keep.tile([P, EXPERTS, WIDE], U32, align_bytes=64)
+        up_words = keep.tile([P, EXPERTS, WIDE], U32, align_bytes=64)
+        down_words = keep.tile([P, EXPERTS, CHUNKS, HIDDEN], U32, align_bytes=64)
+        gate_planes = keep.tile([P, WIDE], U8, align_bytes=64)
+        up_planes = keep.tile([P, WIDE], U8, align_bytes=64)
+        down_planes = keep.tile([P, EXPERTS, HIDDEN], U8, align_bytes=64)
+        out_sb = keep.tile([P, EXPERTS, TOKEN_TILES, HIDDEN], F32)
+        ident_f32 = keep.tile([P, P], F32)
+        ident_bf16 = keep.tile([P, P], BF16)
+        warm_in = keep.tile([P, 1], F32)
+        warm_out = keep.tile([P, 1], F32)
+
+        nc.vector.memset(gate_planes[:].bitcast(I32), 0)
+        nc.vector.memset(up_planes[:].bitcast(I32), 0)
+        nc.vector.memset(down_planes[:].bitcast(I32), 0)
+        nc.vector.memset(warm_in[:], 0.0)
+        nc.scalar.activation(out=warm_out[:], in_=warm_in[:], func=SILU)
+        make_identity(nc, ident_f32[:])
+        make_identity(nc, ident_bf16[:])
+
+        for e in range(EXPERTS):
+            nc.sync.dma_start(
+                out=x_sb[:, e],
+                in_=hidden_states[e * TOKENS : (e + 1) * TOKENS, :].rearrange(
+                    "(p i) k -> p i k", i=TOKEN_TILES
+                ),
+            )
+
+        def load_planes(planes, scales):
+            for quadrant in range(QUADRANTS):
+                nc.sync.dma_start(
+                    out=planes[32 * quadrant : 32 * quadrant + 16, :].bitcast(I32),
+                    in_=scales[:, 4 * quadrant : 4 * quadrant + 4, :].bitcast(I32),
+                )
+
+        load_planes(gate_planes[:], gate_w_scales)
+        load_planes(up_planes[:], up_w_scales)
+        for e in range(EXPERTS):
+            load_planes(down_planes[:, e, :], down_w_scales[e * CHUNKS : (e + 1) * CHUNKS])
+            gate_src = gate_w_words[e].rearrange("p n t -> p (n t)").bitcast(I32)
+            up_src = up_w_words[e].rearrange("p n t -> p (n t)").bitcast(I32)
+            pieces = FIRST_PIECES if e == 0 else 1
+            width = WIDE // pieces
+            for piece in range(pieces):
+                cols = slice(piece * width, (piece + 1) * width)
+                nc.sync.dma_start(out=gate_words[:, e, cols].bitcast(I32), in_=gate_src[:, cols])
+                nc.sync.dma_start(out=up_words[:, e, cols].bitcast(I32), in_=up_src[:, cols])
+            nc.sync.dma_start(
+                out=down_words[:, e].bitcast(I32),
+                in_=down_w_words[e * CHUNKS : (e + 1) * CHUNKS]
+                .rearrange("g p n t -> p g (n t)")
+                .bitcast(I32),
+            )
+
+        x_as_words = x_sb[:].rearrange("p e i k -> p (e i k)").bitcast(F32)
+        words_per_row = HIDDEN // 2
+        for e in range(EXPERTS):
+            x_t = psum.tile([P, TOKEN_TILES, 2, P], F32, tag="transposed")
+            for i in range(TOKEN_TILES):
+                first = (e * TOKEN_TILES + i) * words_per_row
+                for u in range(2):
+                    nc.tensor.transpose(
+                        x_t[:, i, u, :],
+                        x_as_words[:, first + u : first + words_per_row : 2],
+                        ident_f32[:],
+                    )
+            pairs = (
+                x_grouped[:, e]
+                .rearrange("p r t -> p (r t)")
+                .bitcast(F32)
+                .rearrange("p (i r u) -> p i r u", i=TOKEN_TILES, u=2)
+            )
+            if e % 2 == 0:
+                nc.scalar.copy(out=pairs, in_=x_t[:].rearrange("p i u r -> p i r u"))
+            else:
+                nc.vector.tensor_copy(out=pairs, in_=x_t[:].rearrange("p i u r -> p i r u"))
+        for e in range(EXPERTS):
+            nc.vector.quantize_mx(
+                out=x_codes[:, e, :].bitcast(FP8X4),
+                scales=x_scales[:, e, :],
+                in_=x_grouped[:, e].rearrange("p r t -> p (r t)"),
+            )
+
+        def make_h(chunk):
+            e, g = divmod(chunk, CHUNKS)
+            cols = slice(g * K_PASS, (g + 1) * K_PASS)
+            h = work.tile([P, TOKEN_TILES, PACK, P], BF16, tag="h")
+            for i in range(TOKEN_TILES):
+                tokens = slice(i * P, (i + 1) * P)
+                gate_ps = psum.tile([P, K_PASS], F32, tag="gate")
+                up_ps = psum.tile([P, K_PASS], F32, tag="up")
+                for acc, words, planes in (
+                    (gate_ps, gate_words, gate_planes),
+                    (up_ps, up_words, up_planes),
+                ):
+                    nc.tensor.matmul_mx(
+                        out=acc[:],
+                        lhsT=x_codes[:, e, tokens].bitcast(FP8X4),
+                        lhsT_scale=x_scales[:, e, tokens],
+                        rhs=words[:, e, cols].bitcast(FP8X4),
+                        rhs_scale=planes[4 * e : P, cols],
+                        start=True,
+                        stop=True,
+                    )
+                silu = work.tile([P, PACK, P], F32, tag="silu")
+                nc.scalar.activation(
+                    out=silu[:], in_=gate_ps[:].rearrange("p (q t) -> p t q", t=PACK), func=SILU
+                )
+                nc.vector.tensor_tensor(
+                    out=h[:, i],
+                    in0=up_ps[:].rearrange("p (q t) -> p t q", t=PACK),
+                    in1=silu[:],
+                    op=MULT,
+                )
+            return h
+
+        def quantise_h(chunk, h):
+            h_t = psum.tile([P, PACK, TOKENS], BF16, tag="transposed")
+            for i in range(TOKEN_TILES):
+                for t in range(PACK):
+                    nc.tensor.transpose(h_t[:, t, i * P : (i + 1) * P], h[:, i, t, :], ident_bf16[:])
+            grouped = work.tile([P, TOKENS, PACK], BF16, tag="grouped", align_bytes=64)
+            if chunk % 2 == 0:
+                nc.scalar.copy(out=grouped[:], in_=h_t[:].rearrange("p t r -> p r t"))
+            else:
+                nc.vector.tensor_copy(out=grouped[:], in_=h_t[:].rearrange("p t r -> p r t"))
+            codes = work.tile([P, TOKENS], U32, tag="h_codes", align_bytes=64)
+            scales = work.tile([P, TOKENS], U8, tag="h_scales", align_bytes=64)
+            nc.vector.quantize_mx(
+                out=codes[:].bitcast(FP8X4),
+                scales=scales[:],
+                in_=grouped[:].rearrange("p r t -> p (r t)"),
+            )
+            return codes, scales
+
+        def add_to_out(chunk, codes, scales, sums):
+            e, g = divmod(chunk, CHUNKS)
+            for i in range(TOKEN_TILES):
+                tokens = slice(i * P, (i + 1) * P)
+                nc.tensor.matmul_mx(
+                    out=sums[i][:],
+                    lhsT=codes[:, tokens].bitcast(FP8X4),
+                    lhsT_scale=scales[:, tokens],
+                    rhs=down_words[:, e, g, :].bitcast(FP8X4),
+                    rhs_scale=down_planes[4 * g : P, e, :],
+                    start=(g == 0),
+                    stop=(g == CHUNKS - 1),
+                )
+            if g == CHUNKS - 1:
+                rows = out[e * TOKENS : (e + 1) * TOKENS, :].rearrange(
+                    "(p i) n -> p i n", i=TOKEN_TILES
+                )
+                nc.scalar.copy(out=out_sb[:, e, 0, :], in_=sums[0][:])
+                nc.vector.tensor_copy(out=out_sb[:, e, 1, :], in_=sums[1][:])
+                for i in range(TOKEN_TILES):
+                    nc.sync.dma_start(out=rows[:, i, :], in_=out_sb[:, e, i, :])
+
+        n_chunks = EXPERTS * CHUNKS
+        h_of = {}
+        quantised = {}
+        sums = []
+        for step in range(n_chunks + 2):
+            if step < n_chunks:
+                h_of[step] = make_h(step)
+            if 1 <= step <= n_chunks:
+                quantised[step - 1] = quantise_h(step - 1, h_of[step - 1])
+            if step >= 2:
+                chunk = step - 2
+                if chunk % CHUNKS == 0:
+                    sums = [
+                        psum.tile([P, HIDDEN], F32, tag="sums", name="sums%d" % i)
+                        for i in range(TOKEN_TILES)
+                    ]
+                add_to_out(chunk, quantised[chunk][0], quantised[chunk][1], sums)

@@ -40,6 +40,7 @@ def tile_llama4textexperts_e_kernel(
         keep = stack.enter_context(tc.tile_pool(name="keep", bufs=1))
         work = stack.enter_context(tc.tile_pool(name="work", bufs=3))
         psum = stack.enter_context(tc.psum_pool(name="psum", bufs=2))
+        stack.enter_context(tc.manual_schedule())
 
         x_sb = keep.tile([P, EXPERTS, TOKEN_TILES, HIDDEN], BF16)
         x_grouped = keep.tile([P, EXPERTS, TOKENS, PACK], BF16, align_bytes=64)
@@ -102,7 +103,7 @@ def tile_llama4textexperts_e_kernel(
         x_as_words = x_sb[:].rearrange("p e i k -> p (e i k)").bitcast(F32)
         words_per_row = HIDDEN // 2
         for e in range(EXPERTS):
-            x_t = psum.tile([P, TOKEN_TILES, 2, P], F32, tag="transposed")
+            x_t = psum.tile([P, TOKEN_TILES, 2, P], F32, tag="transposed%d" % (e % 2), bufs=1)
             for i in range(TOKEN_TILES):
                 first = (e * TOKEN_TILES + i) * words_per_row
                 for u in range(2):
@@ -162,21 +163,21 @@ def tile_llama4textexperts_e_kernel(
             return h
 
         def quantise_h(chunk, h):
-            h_t = psum.tile([P, PACK, TOKENS], BF16, tag="transposed")
+            grouped = work.tile([P, TOKEN_TILES, P, PACK], BF16, tag="grouped", align_bytes=64)
             for i in range(TOKEN_TILES):
+                h_t = psum.tile([P, PACK, P], BF16, tag="transposed%d" % i, bufs=1)
                 for t in range(PACK):
-                    nc.tensor.transpose(h_t[:, t, i * P : (i + 1) * P], h[:, i, t, :], ident_bf16[:])
-            grouped = work.tile([P, TOKENS, PACK], BF16, tag="grouped", align_bytes=64)
-            if chunk % 2 == 0:
-                nc.scalar.copy(out=grouped[:], in_=h_t[:].rearrange("p t r -> p r t"))
-            else:
-                nc.vector.tensor_copy(out=grouped[:], in_=h_t[:].rearrange("p t r -> p r t"))
+                    nc.tensor.transpose(h_t[:, t, :], h[:, i, t, :], ident_bf16[:])
+                if i == 0:
+                    nc.scalar.copy(out=grouped[:, i], in_=h_t[:].rearrange("p t r -> p r t"))
+                else:
+                    nc.vector.tensor_copy(out=grouped[:, i], in_=h_t[:].rearrange("p t r -> p r t"))
             codes = work.tile([P, TOKENS], U32, tag="h_codes", align_bytes=64)
             scales = work.tile([P, TOKENS], U8, tag="h_scales", align_bytes=64)
             nc.vector.quantize_mx(
                 out=codes[:].bitcast(FP8X4),
                 scales=scales[:],
-                in_=grouped[:].rearrange("p r t -> p (r t)"),
+                in_=grouped[:].rearrange("p i r t -> p (i r t)"),
             )
             return codes, scales
 
@@ -197,22 +198,21 @@ def tile_llama4textexperts_e_kernel(
                 rows = out[e * TOKENS : (e + 1) * TOKENS, :].rearrange(
                     "(p i) n -> p i n", i=TOKEN_TILES
                 )
-                nc.scalar.copy(out=out_sb[:, e, 0, :], in_=sums[0][:])
-                nc.vector.tensor_copy(out=out_sb[:, e, 1, :], in_=sums[1][:])
                 for i in range(TOKEN_TILES):
+                    nc.scalar.copy(out=out_sb[:, e, i, :], in_=sums[i][:])
                     nc.sync.dma_start(out=rows[:, i, :], in_=out_sb[:, e, i, :])
 
         n_chunks = EXPERTS * CHUNKS
         h_of = {}
         quantised = {}
         sums = []
-        for step in range(n_chunks + 2):
+        for step in range(n_chunks + 3):
+            if 2 <= step < n_chunks + 2:
+                quantised[step - 2] = quantise_h(step - 2, h_of[step - 2])
             if step < n_chunks:
                 h_of[step] = make_h(step)
-            if 1 <= step <= n_chunks:
-                quantised[step - 1] = quantise_h(step - 1, h_of[step - 1])
-            if step >= 2:
-                chunk = step - 2
+            if step >= 3:
+                chunk = step - 3
                 if chunk % CHUNKS == 0:
                     sums = [
                         psum.tile([P, HIDDEN], F32, tag="sums", name="sums%d" % i)

@@ -54,7 +54,6 @@ def tile_llama4textexperts_e_kernel(
         down_planes = keep.tile([P, EXPERTS, HIDDEN], U8, align_bytes=64)
         out_sb = keep.tile([P, EXPERTS, TOKEN_TILES, HIDDEN], F32)
         ident_f32 = keep.tile([P, P], F32)
-        ident_bf16 = keep.tile([P, P], BF16)
         warm_in = keep.tile([P, 1], F32)
         warm_out = keep.tile([P, 1], F32)
 
@@ -64,7 +63,6 @@ def tile_llama4textexperts_e_kernel(
         nc.vector.memset(warm_in[:], 0.0)
         nc.scalar.activation(out=warm_out[:], in_=warm_in[:], func=SILU)
         make_identity(nc, ident_f32[:])
-        make_identity(nc, ident_bf16[:])
 
         for e in range(EXPERTS):
             nc.sync.dma_start(
@@ -132,7 +130,7 @@ def tile_llama4textexperts_e_kernel(
         def make_h(chunk):
             e, g = divmod(chunk, CHUNKS)
             cols = slice(g * K_PASS, (g + 1) * K_PASS)
-            h = work.tile([P, TOKEN_TILES, PACK, P], BF16, tag="h")
+            h = work.tile([P, TOKEN_TILES, 2, P, 2], BF16, tag="h")
             for i in range(TOKEN_TILES):
                 tokens = slice(i * P, (i + 1) * P)
                 gate_ps = psum.tile([P, K_PASS], F32, tag="gate")
@@ -150,13 +148,15 @@ def tile_llama4textexperts_e_kernel(
                         start=True,
                         stop=True,
                     )
-                silu = work.tile([P, PACK, P], F32, tag="silu")
+                silu = work.tile([P, 2, P, 2], F32, tag="silu")
                 nc.scalar.activation(
-                    out=silu[:], in_=gate_ps[:].rearrange("p (q t) -> p t q", t=PACK), func=SILU
+                    out=silu[:],
+                    in_=gate_ps[:].rearrange("p (q u j) -> p u q j", u=2, j=2),
+                    func=SILU,
                 )
                 nc.vector.tensor_tensor(
                     out=h[:, i],
-                    in0=up_ps[:].rearrange("p (q t) -> p t q", t=PACK),
+                    in0=up_ps[:].rearrange("p (q u j) -> p u q j", u=2, j=2),
                     in1=silu[:],
                     op=MULT,
                 )
@@ -165,13 +165,23 @@ def tile_llama4textexperts_e_kernel(
         def quantise_h(chunk, h):
             grouped = work.tile([P, TOKEN_TILES, P, PACK], BF16, tag="grouped", align_bytes=64)
             for i in range(TOKEN_TILES):
-                h_t = psum.tile([P, PACK, P], BF16, tag="transposed%d" % i, bufs=1)
-                for t in range(PACK):
-                    nc.tensor.transpose(h_t[:, t, :], h[:, i, t, :], ident_bf16[:])
+                h_t = psum.tile([P, 2, P], F32, tag="transposed%d" % i, bufs=1)
+                for u in range(2):
+                    nc.tensor.transpose(
+                        h_t[:, u, :],
+                        h[:, i, u].rearrange("p q j -> p (q j)").bitcast(F32),
+                        ident_f32[:],
+                    )
+                pairs = (
+                    grouped[:, i]
+                    .rearrange("p r t -> p (r t)")
+                    .bitcast(F32)
+                    .rearrange("p (r u) -> p r u", u=2)
+                )
                 if i == 0:
-                    nc.scalar.copy(out=grouped[:, i], in_=h_t[:].rearrange("p t r -> p r t"))
+                    nc.scalar.copy(out=pairs, in_=h_t[:].rearrange("p u r -> p r u"))
                 else:
-                    nc.vector.tensor_copy(out=grouped[:, i], in_=h_t[:].rearrange("p t r -> p r t"))
+                    nc.vector.tensor_copy(out=pairs, in_=h_t[:].rearrange("p u r -> p r u"))
             codes = work.tile([P, TOKENS], U32, tag="h_codes", align_bytes=64)
             scales = work.tile([P, TOKENS], U8, tag="h_scales", align_bytes=64)
             nc.vector.quantize_mx(

@@ -18,8 +18,10 @@ K_PASS = P * PACK
 EXPERTS, TOKENS, HIDDEN, WIDE = 4, 256, 512, 2048
 TOKEN_TILES = TOKENS // P
 CHUNKS = WIDE // K_PASS
+N_CHUNKS = EXPERTS * CHUNKS
 QUADRANTS = 4
-FIRST_PIECES = 4
+TRANSPOSE_LAG = 2
+MULTIPLY_LAG = 3
 
 FLOPS = 3 * 2 * EXPERTS * TOKENS * HIDDEN * WIDE
 
@@ -43,7 +45,6 @@ def tile_llama4textexperts_e_kernel(
         stack.enter_context(tc.manual_schedule())
 
         x_sb = keep.tile([P, EXPERTS, TOKEN_TILES, HIDDEN], BF16)
-        x_grouped = keep.tile([P, EXPERTS, TOKENS, PACK], BF16, align_bytes=64)
         x_codes = keep.tile([P, EXPERTS, TOKENS], U32, align_bytes=64)
         x_scales = keep.tile([P, EXPERTS, TOKENS], U8, align_bytes=64)
         gate_words = keep.tile([P, EXPERTS, WIDE], U32, align_bytes=64)
@@ -53,7 +54,7 @@ def tile_llama4textexperts_e_kernel(
         up_planes = keep.tile([P, WIDE], U8, align_bytes=64)
         down_planes = keep.tile([P, EXPERTS, HIDDEN], U8, align_bytes=64)
         out_sb = keep.tile([P, EXPERTS, TOKEN_TILES, HIDDEN], F32)
-        ident_f32 = keep.tile([P, P], F32)
+        identity = keep.tile([P, P], F32)
         warm_in = keep.tile([P, 1], F32)
         warm_out = keep.tile([P, 1], F32)
 
@@ -62,9 +63,9 @@ def tile_llama4textexperts_e_kernel(
         nc.vector.memset(down_planes[:].bitcast(I32), 0)
         nc.vector.memset(warm_in[:], 0.0)
         nc.scalar.activation(out=warm_out[:], in_=warm_in[:], func=SILU)
-        make_identity(nc, ident_f32[:])
+        make_identity(nc, identity[:])
 
-        for e in range(EXPERTS):
+        def load_x(e):
             nc.sync.dma_start(
                 out=x_sb[:, e],
                 in_=hidden_states[e * TOKENS : (e + 1) * TOKENS, :].rearrange(
@@ -79,53 +80,56 @@ def tile_llama4textexperts_e_kernel(
                     in_=scales[:, 4 * quadrant : 4 * quadrant + 4, :].bitcast(I32),
                 )
 
+        load_x(0)
         load_planes(gate_planes[:], gate_w_scales)
         load_planes(up_planes[:], up_w_scales)
-        for e in range(EXPERTS):
-            load_planes(down_planes[:, e, :], down_w_scales[e * CHUNKS : (e + 1) * CHUNKS])
-            gate_src = gate_w_words[e].rearrange("p n t -> p (n t)").bitcast(I32)
-            up_src = up_w_words[e].rearrange("p n t -> p (n t)").bitcast(I32)
-            pieces = FIRST_PIECES if e == 0 else 1
-            width = WIDE // pieces
-            for piece in range(pieces):
-                cols = slice(piece * width, (piece + 1) * width)
-                nc.sync.dma_start(out=gate_words[:, e, cols].bitcast(I32), in_=gate_src[:, cols])
-                nc.sync.dma_start(out=up_words[:, e, cols].bitcast(I32), in_=up_src[:, cols])
-            nc.sync.dma_start(
-                out=down_words[:, e].bitcast(I32),
-                in_=down_w_words[e * CHUNKS : (e + 1) * CHUNKS]
-                .rearrange("g p n t -> p g (n t)")
-                .bitcast(I32),
-            )
-
-        x_as_words = x_sb[:].rearrange("p e i k -> p (e i k)").bitcast(F32)
-        words_per_row = HIDDEN // 2
-        for e in range(EXPERTS):
-            x_t = psum.tile([P, TOKEN_TILES, 2, P], F32, tag="transposed%d" % (e % 2), bufs=1)
-            for i in range(TOKEN_TILES):
-                first = (e * TOKEN_TILES + i) * words_per_row
-                for u in range(2):
-                    nc.tensor.transpose(
-                        x_t[:, i, u, :],
-                        x_as_words[:, first + u : first + words_per_row : 2],
-                        ident_f32[:],
+        for step in range(N_CHUNKS + MULTIPLY_LAG):
+            if step < N_CHUNKS:
+                e, g = divmod(step, CHUNKS)
+                if g == CHUNKS - 1 and e + 1 < EXPERTS:
+                    load_x(e + 1)
+                cols = slice(g * K_PASS, (g + 1) * K_PASS)
+                for words, given in ((gate_words, gate_w_words), (up_words, up_w_words)):
+                    nc.sync.dma_start(
+                        out=words[:, e, cols].bitcast(I32),
+                        in_=given[e].rearrange("p n t -> p (n t)").bitcast(I32)[:, cols],
                     )
+            if step >= MULTIPLY_LAG:
+                e, g = divmod(step - MULTIPLY_LAG, CHUNKS)
+                if g == 0:
+                    load_planes(down_planes[:, e, :], down_w_scales[e * CHUNKS : (e + 1) * CHUNKS])
+                nc.sync.dma_start(
+                    out=down_words[:, e, g, :].bitcast(I32),
+                    in_=down_w_words[e * CHUNKS + g].rearrange("p n t -> p (n t)").bitcast(I32),
+                )
+
+        def transpose_words(word_columns):
+            turned = psum.tile([P, TOKEN_TILES, 2, P], F32, tag="turned")
+            for i in range(TOKEN_TILES):
+                for u in range(2):
+                    nc.tensor.transpose(turned[:, i, u, :], word_columns(i, u), identity[:])
+            return turned
+
+        def quantise(turned, codes, scales):
+            grouped = work.tile([P, TOKENS, PACK], BF16, tag="grouped", align_bytes=64)
             pairs = (
-                x_grouped[:, e]
+                grouped[:]
                 .rearrange("p r t -> p (r t)")
                 .bitcast(F32)
                 .rearrange("p (i r u) -> p i r u", i=TOKEN_TILES, u=2)
             )
-            if e % 2 == 0:
-                nc.scalar.copy(out=pairs, in_=x_t[:].rearrange("p i u r -> p i r u"))
-            else:
-                nc.vector.tensor_copy(out=pairs, in_=x_t[:].rearrange("p i u r -> p i r u"))
-        for e in range(EXPERTS):
+            nc.scalar.copy(out=pairs, in_=turned[:].rearrange("p i u r -> p i r u"))
             nc.vector.quantize_mx(
-                out=x_codes[:, e, :].bitcast(FP8X4),
-                scales=x_scales[:, e, :],
-                in_=x_grouped[:, e].rearrange("p r t -> p (r t)"),
+                out=codes.bitcast(FP8X4),
+                scales=scales,
+                in_=grouped[:].rearrange("p r t -> p (r t)"),
             )
+
+        def prepare_x(e):
+            def word_columns(i, u):
+                return x_sb[:, e, i, :].bitcast(F32)[:, u : HIDDEN // 2 : 2]
+
+            quantise(transpose_words(word_columns), x_codes[:, e, :], x_scales[:, e, :])
 
         def make_h(chunk):
             e, g = divmod(chunk, CHUNKS)
@@ -135,12 +139,12 @@ def tile_llama4textexperts_e_kernel(
                 tokens = slice(i * P, (i + 1) * P)
                 gate_ps = psum.tile([P, K_PASS], F32, tag="gate")
                 up_ps = psum.tile([P, K_PASS], F32, tag="up")
-                for acc, words, planes in (
+                for product, words, planes in (
                     (gate_ps, gate_words, gate_planes),
                     (up_ps, up_words, up_planes),
                 ):
                     nc.tensor.matmul_mx(
-                        out=acc[:],
+                        out=product[:],
                         lhsT=x_codes[:, e, tokens].bitcast(FP8X4),
                         lhsT_scale=x_scales[:, e, tokens],
                         rhs=words[:, e, cols].bitcast(FP8X4),
@@ -162,34 +166,11 @@ def tile_llama4textexperts_e_kernel(
                 )
             return h
 
-        def quantise_h(chunk, h):
-            grouped = work.tile([P, TOKEN_TILES, P, PACK], BF16, tag="grouped", align_bytes=64)
-            for i in range(TOKEN_TILES):
-                h_t = psum.tile([P, 2, P], F32, tag="transposed%d" % i, bufs=1)
-                for u in range(2):
-                    nc.tensor.transpose(
-                        h_t[:, u, :],
-                        h[:, i, u].rearrange("p q j -> p (q j)").bitcast(F32),
-                        ident_f32[:],
-                    )
-                pairs = (
-                    grouped[:, i]
-                    .rearrange("p r t -> p (r t)")
-                    .bitcast(F32)
-                    .rearrange("p (r u) -> p r u", u=2)
-                )
-                if i == 0:
-                    nc.scalar.copy(out=pairs, in_=h_t[:].rearrange("p u r -> p r u"))
-                else:
-                    nc.vector.tensor_copy(out=pairs, in_=h_t[:].rearrange("p u r -> p r u"))
-            codes = work.tile([P, TOKENS], U32, tag="h_codes", align_bytes=64)
-            scales = work.tile([P, TOKENS], U8, tag="h_scales", align_bytes=64)
-            nc.vector.quantize_mx(
-                out=codes[:].bitcast(FP8X4),
-                scales=scales[:],
-                in_=grouped[:].rearrange("p i r t -> p (i r t)"),
-            )
-            return codes, scales
+        def transpose_h(h):
+            def word_columns(i, u):
+                return h[:, i, u].rearrange("p q j -> p (q j)").bitcast(F32)
+
+            return transpose_words(word_columns)
 
         def add_to_out(chunk, codes, scales, sums):
             e, g = divmod(chunk, CHUNKS)
@@ -208,24 +189,34 @@ def tile_llama4textexperts_e_kernel(
                 rows = out[e * TOKENS : (e + 1) * TOKENS, :].rearrange(
                     "(p i) n -> p i n", i=TOKEN_TILES
                 )
+                nc.scalar.copy(out=out_sb[:, e, 0, :], in_=sums[0][:])
+                nc.vector.tensor_copy(out=out_sb[:, e, 1, :], in_=sums[1][:])
                 for i in range(TOKEN_TILES):
-                    nc.scalar.copy(out=out_sb[:, e, i, :], in_=sums[i][:])
                     nc.sync.dma_start(out=rows[:, i, :], in_=out_sb[:, e, i, :])
 
-        n_chunks = EXPERTS * CHUNKS
+        prepare_x(0)
         h_of = {}
+        turned_of = {}
         quantised = {}
         sums = []
-        for step in range(n_chunks + 3):
-            if 2 <= step < n_chunks + 2:
-                quantised[step - 2] = quantise_h(step - 2, h_of[step - 2])
-            if step < n_chunks:
+        for step in range(N_CHUNKS + MULTIPLY_LAG):
+            to_turn = step - TRANSPOSE_LAG
+            to_multiply = step - MULTIPLY_LAG
+            if step < N_CHUNKS and step % CHUNKS == CHUNKS - 1 and step + 1 < N_CHUNKS:
+                prepare_x(step // CHUNKS + 1)
+            if 0 <= to_turn < N_CHUNKS:
+                turned_of[to_turn] = transpose_h(h_of[to_turn])
+            if step < N_CHUNKS:
                 h_of[step] = make_h(step)
-            if step >= 3:
-                chunk = step - 3
-                if chunk % CHUNKS == 0:
+            if 0 <= to_turn < N_CHUNKS:
+                codes = work.tile([P, TOKENS], U32, tag="h_codes", align_bytes=64)
+                scales = work.tile([P, TOKENS], U8, tag="h_scales", align_bytes=64)
+                quantise(turned_of[to_turn], codes[:], scales[:])
+                quantised[to_turn] = (codes, scales)
+            if to_multiply >= 0:
+                if to_multiply % CHUNKS == 0:
                     sums = [
                         psum.tile([P, HIDDEN], F32, tag="sums", name="sums%d" % i)
                         for i in range(TOKEN_TILES)
                     ]
-                add_to_out(chunk, quantised[chunk][0], quantised[chunk][1], sums)
+                add_to_out(to_multiply, quantised[to_multiply][0], quantised[to_multiply][1], sums)

@@ -20,8 +20,10 @@ TOKEN_TILES = TOKENS // P
 CHUNKS = WIDE // K_PASS
 N_CHUNKS = EXPERTS * CHUNKS
 QUADRANTS = 4
-TRANSPOSE_LAG = 2
-MULTIPLY_LAG = 3
+GATE_LEAD = 1
+TURN_LAG = 2
+QUANTISE_LAG = 3
+MULTIPLY_LAG = 4
 
 FLOPS = 3 * 2 * EXPERTS * TOKENS * HIDDEN * WIDE
 
@@ -65,11 +67,11 @@ def tile_llama4textexperts_e_kernel(
         nc.scalar.activation(out=warm_out[:], in_=warm_in[:], func=SILU)
         make_identity(nc, identity[:])
 
-        def load_x(e):
+        def load_x(first, last):
             nc.sync.dma_start(
-                out=x_sb[:, e],
-                in_=hidden_states[e * TOKENS : (e + 1) * TOKENS, :].rearrange(
-                    "(p i) k -> p i k", i=TOKEN_TILES
+                out=x_sb[:, first:last].rearrange("p e i k -> p e (i k)"),
+                in_=hidden_states[first * TOKENS : last * TOKENS, :].rearrange(
+                    "(e p i) k -> p e (i k)", p=P, i=TOKEN_TILES
                 ),
             )
 
@@ -80,37 +82,44 @@ def tile_llama4textexperts_e_kernel(
                     in_=scales[:, 4 * quadrant : 4 * quadrant + 4, :].bitcast(I32),
                 )
 
-        load_x(0)
+        def load_columns(words, given, chunk):
+            e, g = divmod(chunk, CHUNKS)
+            cols = slice(g * K_PASS, (g + 1) * K_PASS)
+            nc.sync.dma_start(
+                out=words[:, e, cols].bitcast(I32),
+                in_=given[e].rearrange("p n t -> p (n t)").bitcast(I32)[:, cols],
+            )
+
+        def load_rows(chunk):
+            e, g = divmod(chunk, CHUNKS)
+            if g == 0:
+                load_planes(down_planes[:, e, :], down_w_scales[e * CHUNKS : (e + 1) * CHUNKS])
+            nc.sync.dma_start(
+                out=down_words[:, e, g, :].bitcast(I32),
+                in_=down_w_words[chunk].rearrange("p n t -> p (n t)").bitcast(I32),
+            )
+
+        load_x(0, 1)
+        load_x(1, EXPERTS)
         load_planes(gate_planes[:], gate_w_scales)
+        load_columns(gate_words, gate_w_words, 0)
         load_planes(up_planes[:], up_w_scales)
         for step in range(N_CHUNKS + MULTIPLY_LAG):
+            if step + GATE_LEAD < N_CHUNKS:
+                load_columns(gate_words, gate_w_words, step + GATE_LEAD)
             if step < N_CHUNKS:
-                e, g = divmod(step, CHUNKS)
-                if g == CHUNKS - 1 and e + 1 < EXPERTS:
-                    load_x(e + 1)
-                cols = slice(g * K_PASS, (g + 1) * K_PASS)
-                for words, given in ((gate_words, gate_w_words), (up_words, up_w_words)):
-                    nc.sync.dma_start(
-                        out=words[:, e, cols].bitcast(I32),
-                        in_=given[e].rearrange("p n t -> p (n t)").bitcast(I32)[:, cols],
-                    )
+                load_columns(up_words, up_w_words, step)
             if step >= MULTIPLY_LAG:
-                e, g = divmod(step - MULTIPLY_LAG, CHUNKS)
-                if g == 0:
-                    load_planes(down_planes[:, e, :], down_w_scales[e * CHUNKS : (e + 1) * CHUNKS])
-                nc.sync.dma_start(
-                    out=down_words[:, e, g, :].bitcast(I32),
-                    in_=down_w_words[e * CHUNKS + g].rearrange("p n t -> p (n t)").bitcast(I32),
-                )
+                load_rows(step - MULTIPLY_LAG)
 
-        def transpose_words(word_columns):
-            turned = psum.tile([P, TOKEN_TILES, 2, P], F32, tag="turned")
+        def transpose_words(word_columns, tag):
+            turned = psum.tile([P, TOKEN_TILES, 2, P], F32, tag=tag)
             for i in range(TOKEN_TILES):
                 for u in range(2):
                     nc.tensor.transpose(turned[:, i, u, :], word_columns(i, u), identity[:])
             return turned
 
-        def quantise(turned, codes, scales):
+        def regroup(turned, copy):
             grouped = work.tile([P, TOKENS, PACK], BF16, tag="grouped", align_bytes=64)
             pairs = (
                 grouped[:]
@@ -118,59 +127,72 @@ def tile_llama4textexperts_e_kernel(
                 .bitcast(F32)
                 .rearrange("p (i r u) -> p i r u", i=TOKEN_TILES, u=2)
             )
-            nc.scalar.copy(out=pairs, in_=turned[:].rearrange("p i u r -> p i r u"))
+            copy(out=pairs, in_=turned[:].rearrange("p i u r -> p i r u"))
+            return grouped
+
+        def quantise(grouped, codes, scales):
             nc.vector.quantize_mx(
                 out=codes.bitcast(FP8X4),
                 scales=scales,
                 in_=grouped[:].rearrange("p r t -> p (r t)"),
             )
 
-        def prepare_x(e):
-            def word_columns(i, u):
+        x_grouped = []
+        for e in range(EXPERTS):
+
+            def x_word_columns(i, u, e=e):
                 return x_sb[:, e, i, :].bitcast(F32)[:, u : HIDDEN // 2 : 2]
 
-            quantise(transpose_words(word_columns), x_codes[:, e, :], x_scales[:, e, :])
+            turned = transpose_words(x_word_columns, "turned" if e < 2 else "sums")
+            x_grouped.append(regroup(turned, nc.scalar.copy if e % 2 == 0 else nc.vector.tensor_copy))
+            if e > 0:
+                quantise(x_grouped[e - 1], x_codes[:, e - 1, :], x_scales[:, e - 1, :])
+        quantise(x_grouped[EXPERTS - 1], x_codes[:, EXPERTS - 1, :], x_scales[:, EXPERTS - 1, :])
 
-        def make_h(chunk):
+        def first_layer(product, words, planes, chunk, i):
             e, g = divmod(chunk, CHUNKS)
             cols = slice(g * K_PASS, (g + 1) * K_PASS)
-            h = work.tile([P, TOKEN_TILES, 2, P, 2], BF16, tag="h")
+            tokens = slice(i * P, (i + 1) * P)
+            nc.tensor.matmul_mx(
+                out=product[:],
+                lhsT=x_codes[:, e, tokens].bitcast(FP8X4),
+                lhsT_scale=x_scales[:, e, tokens],
+                rhs=words[:, e, cols].bitcast(FP8X4),
+                rhs_scale=planes[4 * e : P, cols],
+                start=True,
+                stop=True,
+            )
+
+        def make_silu(chunk):
+            silu = work.tile([P, TOKEN_TILES, 2, P, 2], F32, tag="silu")
             for i in range(TOKEN_TILES):
-                tokens = slice(i * P, (i + 1) * P)
                 gate_ps = psum.tile([P, K_PASS], F32, tag="gate")
-                up_ps = psum.tile([P, K_PASS], F32, tag="up")
-                for product, words, planes in (
-                    (gate_ps, gate_words, gate_planes),
-                    (up_ps, up_words, up_planes),
-                ):
-                    nc.tensor.matmul_mx(
-                        out=product[:],
-                        lhsT=x_codes[:, e, tokens].bitcast(FP8X4),
-                        lhsT_scale=x_scales[:, e, tokens],
-                        rhs=words[:, e, cols].bitcast(FP8X4),
-                        rhs_scale=planes[4 * e : P, cols],
-                        start=True,
-                        stop=True,
-                    )
-                silu = work.tile([P, 2, P, 2], F32, tag="silu")
+                first_layer(gate_ps, gate_words, gate_planes, chunk, i)
                 nc.scalar.activation(
-                    out=silu[:],
+                    out=silu[:, i],
                     in_=gate_ps[:].rearrange("p (q u j) -> p u q j", u=2, j=2),
                     func=SILU,
                 )
+            return silu
+
+        def make_h(chunk, silu):
+            h = work.tile([P, TOKEN_TILES, 2, P, 2], BF16, tag="h")
+            for i in range(TOKEN_TILES):
+                up_ps = psum.tile([P, K_PASS], F32, tag="up")
+                first_layer(up_ps, up_words, up_planes, chunk, i)
                 nc.vector.tensor_tensor(
                     out=h[:, i],
                     in0=up_ps[:].rearrange("p (q u j) -> p u q j", u=2, j=2),
-                    in1=silu[:],
+                    in1=silu[:, i],
                     op=MULT,
                 )
             return h
 
         def transpose_h(h):
-            def word_columns(i, u):
+            def h_word_columns(i, u):
                 return h[:, i, u].rearrange("p q j -> p (q j)").bitcast(F32)
 
-            return transpose_words(word_columns)
+            return transpose_words(h_word_columns, "turned")
 
         def add_to_out(chunk, codes, scales, sums):
             e, g = divmod(chunk, CHUNKS)
@@ -194,25 +216,27 @@ def tile_llama4textexperts_e_kernel(
                 for i in range(TOKEN_TILES):
                     nc.sync.dma_start(out=rows[:, i, :], in_=out_sb[:, e, i, :])
 
-        prepare_x(0)
+        silu_of = {0: make_silu(0)}
         h_of = {}
         turned_of = {}
+        grouped_of = {}
         quantised = {}
         sums = []
         for step in range(N_CHUNKS + MULTIPLY_LAG):
-            to_turn = step - TRANSPOSE_LAG
+            to_turn = step - TURN_LAG
+            to_quantise = step - QUANTISE_LAG
             to_multiply = step - MULTIPLY_LAG
-            if step < N_CHUNKS and step % CHUNKS == CHUNKS - 1 and step + 1 < N_CHUNKS:
-                prepare_x(step // CHUNKS + 1)
             if 0 <= to_turn < N_CHUNKS:
                 turned_of[to_turn] = transpose_h(h_of[to_turn])
-            if step < N_CHUNKS:
-                h_of[step] = make_h(step)
-            if 0 <= to_turn < N_CHUNKS:
+            if 0 <= to_quantise < N_CHUNKS:
                 codes = work.tile([P, TOKENS], U32, tag="h_codes", align_bytes=64)
                 scales = work.tile([P, TOKENS], U8, tag="h_scales", align_bytes=64)
-                quantise(turned_of[to_turn], codes[:], scales[:])
-                quantised[to_turn] = (codes, scales)
+                quantise(grouped_of[to_quantise], codes[:], scales[:])
+                quantised[to_quantise] = (codes, scales)
+            if step + GATE_LEAD < N_CHUNKS:
+                silu_of[step + GATE_LEAD] = make_silu(step + GATE_LEAD)
+            if step < N_CHUNKS:
+                h_of[step] = make_h(step, silu_of[step])
             if to_multiply >= 0:
                 if to_multiply % CHUNKS == 0:
                     sums = [
@@ -220,3 +244,5 @@ def tile_llama4textexperts_e_kernel(
                         for i in range(TOKEN_TILES)
                     ]
                 add_to_out(to_multiply, quantised[to_multiply][0], quantised[to_multiply][1], sums)
+            if 0 <= to_turn < N_CHUNKS:
+                grouped_of[to_turn] = regroup(turned_of[to_turn], nc.scalar.copy)

@@ -20,10 +20,8 @@ TOKEN_TILES = TOKENS // P
 CHUNKS = WIDE // K_PASS
 N_CHUNKS = EXPERTS * CHUNKS
 QUADRANTS = 4
-GATE_LEAD = 1
-TURN_LAG = 2
-QUANTISE_LAG = 3
-MULTIPLY_LAG = 4
+RUN = 2
+N_ROUNDS = N_CHUNKS // RUN
 
 FLOPS = 3 * 2 * EXPERTS * TOKENS * HIDDEN * WIDE
 
@@ -104,13 +102,15 @@ def tile_llama4textexperts_e_kernel(
         load_planes(gate_planes[:], gate_w_scales)
         load_columns(gate_words, gate_w_words, 0)
         load_planes(up_planes[:], up_w_scales)
-        for step in range(N_CHUNKS + MULTIPLY_LAG):
-            if step + GATE_LEAD < N_CHUNKS:
-                load_columns(gate_words, gate_w_words, step + GATE_LEAD)
-            if step < N_CHUNKS:
-                load_columns(up_words, up_w_words, step)
-            if step >= MULTIPLY_LAG:
-                load_rows(step - MULTIPLY_LAG)
+        for round_ in range(N_ROUNDS + 2):
+            for chunk in range(round_ * RUN, (round_ + 1) * RUN):
+                if chunk + 1 < N_CHUNKS:
+                    load_columns(gate_words, gate_w_words, chunk + 1)
+                if chunk < N_CHUNKS:
+                    load_columns(up_words, up_w_words, chunk)
+            for chunk in range((round_ - 2) * RUN, (round_ - 1) * RUN):
+                if chunk >= 0:
+                    load_rows(chunk)
 
         def transpose_words(word_columns, tag):
             turned = psum.tile([P, TOKEN_TILES, 2, P], F32, tag=tag)
@@ -120,7 +120,7 @@ def tile_llama4textexperts_e_kernel(
             return turned
 
         def regroup(turned, copy):
-            grouped = work.tile([P, TOKENS, PACK], BF16, tag="grouped", align_bytes=64)
+            grouped = work.tile([P, TOKENS, PACK], BF16, tag="grouped", bufs=4, align_bytes=64)
             pairs = (
                 grouped[:]
                 .rearrange("p r t -> p (r t)")
@@ -218,31 +218,35 @@ def tile_llama4textexperts_e_kernel(
 
         silu_of = {0: make_silu(0)}
         h_of = {}
-        turned_of = {}
-        grouped_of = {}
         quantised = {}
-        sums = []
-        for step in range(N_CHUNKS + MULTIPLY_LAG):
-            to_turn = step - TURN_LAG
-            to_quantise = step - QUANTISE_LAG
-            to_multiply = step - MULTIPLY_LAG
-            if 0 <= to_turn < N_CHUNKS:
-                turned_of[to_turn] = transpose_h(h_of[to_turn])
-            if 0 <= to_quantise < N_CHUNKS:
-                codes = work.tile([P, TOKENS], U32, tag="h_codes", align_bytes=64)
-                scales = work.tile([P, TOKENS], U8, tag="h_scales", align_bytes=64)
-                quantise(grouped_of[to_quantise], codes[:], scales[:])
-                quantised[to_quantise] = (codes, scales)
-            if step + GATE_LEAD < N_CHUNKS:
-                silu_of[step + GATE_LEAD] = make_silu(step + GATE_LEAD)
-            if step < N_CHUNKS:
-                h_of[step] = make_h(step, silu_of[step])
-            if to_multiply >= 0:
-                if to_multiply % CHUNKS == 0:
-                    sums = [
-                        psum.tile([P, HIDDEN], F32, tag="sums", name="sums%d" % i)
-                        for i in range(TOKEN_TILES)
-                    ]
-                add_to_out(to_multiply, quantised[to_multiply][0], quantised[to_multiply][1], sums)
-            if 0 <= to_turn < N_CHUNKS:
-                grouped_of[to_turn] = regroup(turned_of[to_turn], nc.scalar.copy)
+
+        def make(chunk):
+            if chunk + 1 < N_CHUNKS:
+                silu_of[chunk + 1] = make_silu(chunk + 1)
+            if chunk < N_CHUNKS:
+                h_of[chunk] = make_h(chunk, silu_of[chunk])
+
+        for round_ in range(N_ROUNDS + 2):
+            first, second = round_ * RUN, round_ * RUN + 1
+            to_quantise = 1 <= round_ <= N_ROUNDS
+            make(first)
+            if to_quantise:
+                turned_first = transpose_h(h_of[first - RUN])
+                turned_second = transpose_h(h_of[second - RUN])
+                grouped_first = regroup(turned_first, nc.scalar.copy)
+                grouped_second = regroup(turned_second, nc.vector.tensor_copy)
+            make(second)
+            if to_quantise:
+                for chunk, grouped in ((first - RUN, grouped_first), (second - RUN, grouped_second)):
+                    codes = work.tile([P, TOKENS], U32, tag="h_codes", bufs=4, align_bytes=64)
+                    scales = work.tile([P, TOKENS], U8, tag="h_scales", bufs=4, align_bytes=64)
+                    quantise(grouped, codes[:], scales[:])
+                    quantised[chunk] = (codes, scales)
+            if round_ >= 2:
+                for chunk in (first - 2 * RUN, second - 2 * RUN):
+                    if chunk % CHUNKS == 0:
+                        sums = [
+                            psum.tile([P, HIDDEN], F32, tag="sums", name="sums%d" % i)
+                            for i in range(TOKEN_TILES)
+                        ]
+                    add_to_out(chunk, quantised[chunk][0], quantised[chunk][1], sums)

@@ -163,30 +163,24 @@ def tile_llama4textexperts_e_kernel(
                 stop=True,
             )
 
-        def make_silu(chunk):
-            silu = work.tile([P, TOKEN_TILES, 2, P, 2], F32, tag="silu")
-            for i in range(TOKEN_TILES):
-                gate_ps = psum.tile([P, K_PASS], F32, tag="gate")
-                first_layer(gate_ps, gate_words, gate_planes, chunk, i)
-                nc.scalar.activation(
-                    out=silu[:, i],
-                    in_=gate_ps[:].rearrange("p (q u j) -> p u q j", u=2, j=2),
-                    func=SILU,
-                )
-            return silu
+        def make_silu(silu, chunk, i):
+            gate_ps = psum.tile([P, K_PASS], F32, tag="gate")
+            first_layer(gate_ps, gate_words, gate_planes, chunk, i)
+            nc.scalar.activation(
+                out=silu[:, i],
+                in_=gate_ps[:].rearrange("p (q u j) -> p u q j", u=2, j=2),
+                func=SILU,
+            )
 
-        def make_h(chunk, silu):
-            h = work.tile([P, TOKEN_TILES, 2, P, 2], BF16, tag="h")
-            for i in range(TOKEN_TILES):
-                up_ps = psum.tile([P, K_PASS], F32, tag="up")
-                first_layer(up_ps, up_words, up_planes, chunk, i)
-                nc.vector.tensor_tensor(
-                    out=h[:, i],
-                    in0=up_ps[:].rearrange("p (q u j) -> p u q j", u=2, j=2),
-                    in1=silu[:, i],
-                    op=MULT,
-                )
-            return h
+        def make_h(h, silu, chunk, i):
+            up_ps = psum.tile([P, K_PASS], F32, tag="up")
+            first_layer(up_ps, up_words, up_planes, chunk, i)
+            nc.vector.tensor_tensor(
+                out=h[:, i],
+                in0=up_ps[:].rearrange("p (q u j) -> p u q j", u=2, j=2),
+                in1=silu[:, i],
+                op=MULT,
+            )
 
         def transpose_h(h):
             def h_word_columns(i, u):
@@ -216,16 +210,22 @@ def tile_llama4textexperts_e_kernel(
                 for i in range(TOKEN_TILES):
                     nc.sync.dma_start(out=rows[:, i, :], in_=out_sb[:, e, i, :])
 
-        silu_of = {0: make_silu(0)}
+        silu_of = {}
         h_of = {}
         quantised = {}
 
         def make(chunk):
             if chunk + 1 < N_CHUNKS:
-                silu_of[chunk + 1] = make_silu(chunk + 1)
-            if chunk < N_CHUNKS:
-                h_of[chunk] = make_h(chunk, silu_of[chunk])
+                silu_of[chunk + 1] = work.tile([P, TOKEN_TILES, 2, P, 2], F32, tag="silu", name="silu")
+            if 0 <= chunk < N_CHUNKS:
+                h_of[chunk] = work.tile([P, TOKEN_TILES, 2, P, 2], BF16, tag="h", name="h")
+            for i in range(TOKEN_TILES):
+                if chunk + 1 < N_CHUNKS:
+                    make_silu(silu_of[chunk + 1], chunk + 1, i)
+                if 0 <= chunk < N_CHUNKS:
+                    make_h(h_of[chunk], silu_of[chunk], chunk, i)
 
+        make(-1)
         for round_ in range(N_ROUNDS + 2):
             first, second = round_ * RUN, round_ * RUN + 1
             to_quantise = 1 <= round_ <= N_ROUNDS

@@ -55,14 +55,10 @@ def tile_llama4textexperts_e_kernel(
         down_planes = keep.tile([P, EXPERTS, HIDDEN], U8, align_bytes=64)
         out_sb = keep.tile([P, EXPERTS, TOKEN_TILES, HIDDEN], F32)
         identity = keep.tile([P, P], F32)
-        warm_in = keep.tile([P, 1], F32)
-        warm_out = keep.tile([P, 1], F32)
 
         nc.vector.memset(gate_planes[:].bitcast(I32), 0)
         nc.vector.memset(up_planes[:].bitcast(I32), 0)
         nc.vector.memset(down_planes[:].bitcast(I32), 0)
-        nc.vector.memset(warm_in[:], 0.0)
-        nc.scalar.activation(out=warm_out[:], in_=warm_in[:], func=SILU)
         make_identity(nc, identity[:])
 
         def load_x(first, last):

@@ -56,6 +56,9 @@ def tile_llama4textexperts_e_kernel(
         out_sb = keep.tile([P, EXPERTS, TOKEN_TILES, HIDDEN], F32)
         identity = keep.tile([P, P], F32)
 
+        warm = keep.tile([P, 2], F32)
+        nc.vector.memset(warm[:, 0:1], 0.0)
+        nc.scalar.activation(out=warm[:, 1:2], in_=warm[:, 0:1], func=SILU)
         nc.vector.memset(gate_planes[:].bitcast(I32), 0)
         nc.vector.memset(up_planes[:].bitcast(I32), 0)
         nc.vector.memset(down_planes[:].bitcast(I32), 0)
@@ -93,8 +96,11 @@ def tile_llama4textexperts_e_kernel(
                 in_=down_w_words[chunk].rearrange("p n t -> p (n t)").bitcast(I32),
             )
 
+        def expert_turned_in(round_):
+            e = round_ // 2 + 1
+            return e if round_ % 2 == 0 and e < EXPERTS else None
+
         load_x(0, 1)
-        load_x(1, EXPERTS)
         load_planes(gate_planes[:], gate_w_scales)
         load_columns(gate_words, gate_w_words, 0)
         load_planes(up_planes[:], up_w_scales)
@@ -104,6 +110,8 @@ def tile_llama4textexperts_e_kernel(
                     load_columns(gate_words, gate_w_words, chunk + 1)
                 if chunk < N_CHUNKS:
                     load_columns(up_words, up_w_words, chunk)
+                if chunk == round_ * RUN and expert_turned_in(round_) is not None:
+                    load_x(expert_turned_in(round_), expert_turned_in(round_) + 1)
             for chunk in range((round_ - 2) * RUN, (round_ - 1) * RUN):
                 if chunk >= 0:
                     load_rows(chunk)
@@ -133,17 +141,16 @@ def tile_llama4textexperts_e_kernel(
                 in_=grouped[:].rearrange("p r t -> p (r t)"),
             )
 
-        x_grouped = []
-        for e in range(EXPERTS):
-
-            def x_word_columns(i, u, e=e):
+        def transpose_x(e):
+            def x_word_columns(i, u):
                 return x_sb[:, e, i, :].bitcast(F32)[:, u : HIDDEN // 2 : 2]
 
-            turned = transpose_words(x_word_columns, "turned" if e < 2 else "sums")
-            x_grouped.append(regroup(turned, nc.scalar.copy if e % 2 == 0 else nc.vector.tensor_copy))
-            if e > 0:
-                quantise(x_grouped[e - 1], x_codes[:, e - 1, :], x_scales[:, e - 1, :])
-        quantise(x_grouped[EXPERTS - 1], x_codes[:, EXPERTS - 1, :], x_scales[:, EXPERTS - 1, :])
+            return regroup(transpose_words(x_word_columns, "sums"), nc.scalar.copy)
+
+        def quantise_x(e, grouped):
+            quantise(grouped, x_codes[:, e, :], x_scales[:, e, :])
+
+        quantise_x(0, transpose_x(0))
 
         def first_layer(product, words, planes, chunk, i):
             e, g = divmod(chunk, CHUNKS)
@@ -226,12 +233,17 @@ def tile_llama4textexperts_e_kernel(
             first, second = round_ * RUN, round_ * RUN + 1
             to_quantise = 1 <= round_ <= N_ROUNDS
             make(first)
+            next_expert = expert_turned_in(round_)
+            if next_expert is not None:
+                x_grouped = transpose_x(next_expert)
             if to_quantise:
                 turned_first = transpose_h(h_of[first - RUN])
                 turned_second = transpose_h(h_of[second - RUN])
                 grouped_first = regroup(turned_first, nc.scalar.copy)
                 grouped_second = regroup(turned_second, nc.vector.tensor_copy)
             make(second)
+            if next_expert is not None:
+                quantise_x(next_expert, x_grouped)
             if to_quantise:
                 for chunk, grouped in ((first - RUN, grouped_first), (second - RUN, grouped_second)):
                     codes = work.tile([P, TOKENS], U32, tag="h_codes", bufs=4, align_bytes=64)

@@ -103,13 +103,14 @@ def tile_llama4textexperts_e_kernel(
         load_x(0, 1)
         load_planes(gate_planes[:], gate_w_scales)
         load_columns(gate_words, gate_w_words, 0)
-        load_planes(up_planes[:], up_w_scales)
         for round_ in range(N_ROUNDS + 2):
             for chunk in range(round_ * RUN, (round_ + 1) * RUN):
                 if chunk + 1 < N_CHUNKS:
                     load_columns(gate_words, gate_w_words, chunk + 1)
                 if chunk < N_CHUNKS:
                     load_columns(up_words, up_w_words, chunk)
+                if chunk == 0:
+                    load_planes(up_planes[:], up_w_scales)
                 if chunk == round_ * RUN and expert_turned_in(round_) is not None:
                     load_x(expert_turned_in(round_), expert_turned_in(round_) + 1)
             for chunk in range((round_ - 2) * RUN, (round_ - 1) * RUN):
@@ -141,16 +142,32 @@ def tile_llama4textexperts_e_kernel(
                 in_=grouped[:].rearrange("p r t -> p (r t)"),
             )
 
+        def x_words(e, i, u):
+            return x_sb[:, e, i, :].bitcast(F32)[:, u : HIDDEN // 2 : 2]
+
         def transpose_x(e):
             def x_word_columns(i, u):
-                return x_sb[:, e, i, :].bitcast(F32)[:, u : HIDDEN // 2 : 2]
+                return x_words(e, i, u)
 
             return regroup(transpose_words(x_word_columns, "sums"), nc.scalar.copy)
 
         def quantise_x(e, grouped):
             quantise(grouped, x_codes[:, e, :], x_scales[:, e, :])
 
-        quantise_x(0, transpose_x(0))
+        x0_grouped = []
+        for i in range(TOKEN_TILES):
+            x0_turned = psum.tile([P, 2, P], F32, tag="sums")
+            for u in range(2):
+                nc.tensor.transpose(x0_turned[:, u, :], x_words(0, i, u), identity[:])
+            x0_tile = work.tile([P, P, PACK], BF16, tag="grouped", bufs=4, align_bytes=64)
+            nc.scalar.copy(
+                out=x0_tile[:].rearrange("p r t -> p (r t)").bitcast(F32).rearrange("p (r u) -> p r u", u=2),
+                in_=x0_turned[:].rearrange("p u r -> p r u"),
+            )
+            x0_grouped.append(x0_tile)
+        for i in range(TOKEN_TILES):
+            tokens = slice(i * P, (i + 1) * P)
+            quantise(x0_grouped[i], x_codes[:, 0, tokens], x_scales[:, 0, tokens])
 
         def first_layer(product, words, planes, chunk, i):
             e, g = divmod(chunk, CHUNKS)
@@ -191,10 +208,11 @@ def tile_llama4textexperts_e_kernel(
 
             return transpose_words(h_word_columns, "turned")
 
-        def add_to_out(chunk, codes, scales, sums):
-            e, g = divmod(chunk, CHUNKS)
-            for i in range(TOKEN_TILES):
-                tokens = slice(i * P, (i + 1) * P)
+        def add_to_out(chunks, i, sums):
+            tokens = slice(i * P, (i + 1) * P)
+            for chunk in chunks:
+                e, g = divmod(chunk, CHUNKS)
+                codes, scales = quantised[chunk]
                 nc.tensor.matmul_mx(
                     out=sums[i][:],
                     lhsT=codes[:, tokens].bitcast(FP8X4),
@@ -208,10 +226,8 @@ def tile_llama4textexperts_e_kernel(
                 rows = out[e * TOKENS : (e + 1) * TOKENS, :].rearrange(
                     "(p i) n -> p i n", i=TOKEN_TILES
                 )
-                nc.scalar.copy(out=out_sb[:, e, 0, :], in_=sums[0][:])
-                nc.vector.tensor_copy(out=out_sb[:, e, 1, :], in_=sums[1][:])
-                for i in range(TOKEN_TILES):
-                    nc.sync.dma_start(out=rows[:, i, :], in_=out_sb[:, e, i, :])
+                nc.scalar.copy(out=out_sb[:, e, i, :], in_=sums[i][:])
+                nc.sync.dma_start(out=rows[:, i, :], in_=out_sb[:, e, i, :])
 
         silu_of = {}
         h_of = {}
@@ -251,10 +267,10 @@ def tile_llama4textexperts_e_kernel(
                     quantise(grouped, codes[:], scales[:])
                     quantised[chunk] = (codes, scales)
             if round_ >= 2:
-                for chunk in (first - 2 * RUN, second - 2 * RUN):
-                    if chunk % CHUNKS == 0:
-                        sums = [
-                            psum.tile([P, HIDDEN], F32, tag="sums", name="sums%d" % i)
-                            for i in range(TOKEN_TILES)
-                        ]
-                    add_to_out(chunk, quantised[chunk][0], quantised[chunk][1], sums)
+                if (first - 2 * RUN) % CHUNKS == 0:
+                    sums = [
+                        psum.tile([P, HIDDEN], F32, tag="sums", name="sums%d" % i)
+                        for i in range(TOKEN_TILES)
+                    ]
+                for i in range(TOKEN_TILES):
+                    add_to_out((first - 2 * RUN, second - 2 * RUN), i, sums)

@@ -53,12 +53,16 @@ def tile_llama4textexperts_e_kernel(
         gate_planes = keep.tile([P, WIDE], U8, align_bytes=64)
         up_planes = keep.tile([P, WIDE], U8, align_bytes=64)
         down_planes = keep.tile([P, EXPERTS, HIDDEN], U8, align_bytes=64)
+        gate_planes_0 = keep.tile([P, WIDE], U8, align_bytes=64)
+        up_planes_0 = keep.tile([P, WIDE], U8, align_bytes=64)
         out_sb = keep.tile([P, EXPERTS, TOKEN_TILES, HIDDEN], F32)
         identity = keep.tile([P, P], F32)
 
         warm = keep.tile([P, 2], F32)
         nc.vector.memset(warm[:, 0:1], 0.0)
         nc.scalar.activation(out=warm[:, 1:2], in_=warm[:, 0:1], func=SILU)
+        nc.vector.memset(gate_planes_0[:].bitcast(I32), 0)
+        nc.vector.memset(up_planes_0[:].bitcast(I32), 0)
         nc.vector.memset(gate_planes[:].bitcast(I32), 0)
         nc.vector.memset(up_planes[:].bitcast(I32), 0)
         nc.vector.memset(down_planes[:].bitcast(I32), 0)
@@ -77,6 +81,20 @@ def tile_llama4textexperts_e_kernel(
                 nc.sync.dma_start(
                     out=planes[32 * quadrant : 32 * quadrant + 16, :].bitcast(I32),
                     in_=scales[:, 4 * quadrant : 4 * quadrant + 4, :].bitcast(I32),
+                )
+
+        def load_planes_of_expert_0(planes, scales):
+            for quadrant in range(QUADRANTS):
+                nc.sync.dma_start(
+                    out=planes[32 * quadrant : 32 * quadrant + 4, :].bitcast(I32),
+                    in_=scales[0, 4 * quadrant : 4 * quadrant + 4, :].bitcast(I32),
+                )
+
+        def load_packed_planes_aside(planes, scales):
+            for quadrant in range(QUADRANTS):
+                nc.gpsimd.dma_start(
+                    out=planes[32 * quadrant : 32 * quadrant + 16, :].bitcast(F32),
+                    in_=scales[:, 4 * quadrant : 4 * quadrant + 4, :].bitcast(F32),
                 )
 
         def load_columns(words, given, chunk):
@@ -100,8 +118,10 @@ def tile_llama4textexperts_e_kernel(
             e = round_ // 2 + 1
             return e if round_ % 2 == 0 and e < EXPERTS else None
 
+        load_packed_planes_aside(gate_planes[:], gate_w_scales)
+        load_packed_planes_aside(up_planes[:], up_w_scales)
         load_x(0, 1)
-        load_planes(gate_planes[:], gate_w_scales)
+        load_planes_of_expert_0(gate_planes_0, gate_w_scales)
         load_columns(gate_words, gate_w_words, 0)
         for round_ in range(N_ROUNDS + 2):
             for chunk in range(round_ * RUN, (round_ + 1) * RUN):
@@ -110,7 +130,7 @@ def tile_llama4textexperts_e_kernel(
                 if chunk < N_CHUNKS:
                     load_columns(up_words, up_w_words, chunk)
                 if chunk == 0:
-                    load_planes(up_planes[:], up_w_scales)
+                    load_planes_of_expert_0(up_planes_0, up_w_scales)
                 if chunk == round_ * RUN and expert_turned_in(round_) is not None:
                     load_x(expert_turned_in(round_), expert_turned_in(round_) + 1)
             for chunk in range((round_ - 2) * RUN, (round_ - 1) * RUN):
@@ -169,7 +189,7 @@ def tile_llama4textexperts_e_kernel(
             tokens = slice(i * P, (i + 1) * P)
             quantise(x0_grouped[i], x_codes[:, 0, tokens], x_scales[:, 0, tokens])
 
-        def first_layer(product, words, planes, chunk, i):
+        def first_layer(product, words, planes_0, planes, chunk, i):
             e, g = divmod(chunk, CHUNKS)
             cols = slice(g * K_PASS, (g + 1) * K_PASS)
             tokens = slice(i * P, (i + 1) * P)
@@ -178,14 +198,14 @@ def tile_llama4textexperts_e_kernel(
                 lhsT=x_codes[:, e, tokens].bitcast(FP8X4),
                 lhsT_scale=x_scales[:, e, tokens],
                 rhs=words[:, e, cols].bitcast(FP8X4),
-                rhs_scale=planes[4 * e : P, cols],
+                rhs_scale=planes_0[:, cols] if e == 0 else planes[4 * e : P, cols],
                 start=True,
                 stop=True,
             )
 
         def make_silu(silu, chunk, i):
             gate_ps = psum.tile([P, K_PASS], F32, tag="gate")
-            first_layer(gate_ps, gate_words, gate_planes, chunk, i)
+            first_layer(gate_ps, gate_words, gate_planes_0, gate_planes, chunk, i)
             nc.scalar.activation(
                 out=silu[:, i],
                 in_=gate_ps[:].rearrange("p (q u j) -> p u q j", u=2, j=2),
@@ -194,7 +214,7 @@ def tile_llama4textexperts_e_kernel(
 
         def make_h(h, silu, chunk, i):
             up_ps = psum.tile([P, K_PASS], F32, tag="up")
-            first_layer(up_ps, up_words, up_planes, chunk, i)
+            first_layer(up_ps, up_words, up_planes_0, up_planes, chunk, i)
             nc.vector.tensor_tensor(
                 out=h[:, i],
                 in0=up_ps[:].rearrange("p (q u j) -> p u q j", u=2, j=2),

@@ -62,8 +62,8 @@ def tile_llama4textexperts_e_kernel(
         nc.vector.memset(warm[:, 0:1], 0.0)
         nc.scalar.activation(out=warm[:, 1:2], in_=warm[:, 0:1], func=SILU)
         nc.vector.memset(gate_planes_0[:].bitcast(I32), 0)
-        nc.vector.memset(up_planes_0[:].bitcast(I32), 0)
         nc.vector.memset(gate_planes[:].bitcast(I32), 0)
+        nc.vector.memset(up_planes_0[:].bitcast(I32), 0)
         nc.vector.memset(up_planes[:].bitcast(I32), 0)
         nc.vector.memset(down_planes[:].bitcast(I32), 0)
         make_identity(nc, identity[:])
@@ -228,26 +228,31 @@ def tile_llama4textexperts_e_kernel(
 
             return transpose_words(h_word_columns, "turned")
 
-        def add_to_out(chunks, i, sums):
+        def add_to_out(chunks, i, pieces):
             tokens = slice(i * P, (i + 1) * P)
             for chunk in chunks:
                 e, g = divmod(chunk, CHUNKS)
                 codes, scales = quantised[chunk]
-                nc.tensor.matmul_mx(
-                    out=sums[i][:],
-                    lhsT=codes[:, tokens].bitcast(FP8X4),
-                    lhsT_scale=scales[:, tokens],
-                    rhs=down_words[:, e, g, :].bitcast(FP8X4),
-                    rhs_scale=down_planes[4 * g : P, e, :],
-                    start=(g == 0),
-                    stop=(g == CHUNKS - 1),
-                )
+                for sums, cols in pieces:
+                    nc.tensor.matmul_mx(
+                        out=sums[:],
+                        lhsT=codes[:, tokens].bitcast(FP8X4),
+                        lhsT_scale=scales[:, tokens],
+                        rhs=down_words[:, e, g, cols].bitcast(FP8X4),
+                        rhs_scale=down_planes[4 * g : P, e, cols],
+                        start=(g == 0),
+                        stop=(g == CHUNKS - 1),
+                    )
             if g == CHUNKS - 1:
                 rows = out[e * TOKENS : (e + 1) * TOKENS, :].rearrange(
                     "(p i) n -> p i n", i=TOKEN_TILES
                 )
-                nc.scalar.copy(out=out_sb[:, e, i, :], in_=sums[i][:])
-                nc.sync.dma_start(out=rows[:, i, :], in_=out_sb[:, e, i, :])
+                for sums, cols in pieces[:-1]:
+                    nc.vector.tensor_copy(out=out_sb[:, e, i, cols], in_=sums[:])
+                    nc.sync.dma_start(out=rows[:, i, cols], in_=out_sb[:, e, i, cols])
+                sums, cols = pieces[-1]
+                nc.scalar.copy(out=out_sb[:, e, i, cols], in_=sums[:])
+                nc.sync.dma_start(out=rows[:, i, cols], in_=out_sb[:, e, i, cols])
 
         silu_of = {}
         h_of = {}
@@ -288,9 +293,15 @@ def tile_llama4textexperts_e_kernel(
                     quantised[chunk] = (codes, scales)
             if round_ >= 2:
                 if (first - 2 * RUN) % CHUNKS == 0:
-                    sums = [
-                        psum.tile([P, HIDDEN], F32, tag="sums", name="sums%d" % i)
+                    pieces_of = [
+                        [(psum.tile([P, HIDDEN], F32, tag="sums", name="sums%d" % i), slice(0, HIDDEN))]
                         for i in range(TOKEN_TILES)
                     ]
+                    if first - 2 * RUN == N_CHUNKS - CHUNKS:
+                        half = HIDDEN // 2
+                        pieces_of[1] = [
+                            (pieces_of[1][0][0][:, 0:half], slice(0, half)),
+                            (psum.tile([P, half], F32, tag="gate", name="sums_half"), slice(half, HIDDEN)),
+                        ]
                 for i in range(TOKEN_TILES):
-                    add_to_out((first - 2 * RUN, second - 2 * RUN), i, sums)
+                    add_to_out((first - 2 * RUN, second - 2 * RUN), i, pieces_of[i])

@@ -22,6 +22,7 @@ N_CHUNKS = EXPERTS * CHUNKS
 QUADRANTS = 4
 RUN = 2
 N_ROUNDS = N_CHUNKS // RUN
+GATE_BANKS = {1: "turned", 3: "sums"}
 
 FLOPS = 3 * 2 * EXPERTS * TOKENS * HIDDEN * WIDE
 
@@ -204,7 +205,7 @@ def tile_llama4textexperts_e_kernel(
             )
 
         def make_silu(silu, chunk, i):
-            gate_ps = psum.tile([P, K_PASS], F32, tag="gate")
+            gate_ps = psum.tile([P, K_PASS], F32, tag=GATE_BANKS.get(chunk, "gate"), name="gate_ps")
             first_layer(gate_ps, gate_words, gate_planes_0, gate_planes, chunk, i)
             nc.scalar.activation(
                 out=silu[:, i],

@@ -60,10 +60,10 @@ def tile_llama4textexperts_e_kernel(
         identity = keep.tile([P, P], F32)
 
         warm = keep.tile([P, 2], F32)
-        nc.vector.memset(warm[:, 0:1], 0.0)
-        nc.scalar.activation(out=warm[:, 1:2], in_=warm[:, 0:1], func=SILU)
         nc.vector.memset(gate_planes_0[:].bitcast(I32), 0)
         nc.vector.memset(gate_planes[:].bitcast(I32), 0)
+        nc.vector.memset(warm[:, 0:1], 0.0)
+        nc.scalar.activation(out=warm[:, 1:2], in_=warm[:, 0:1], func=SILU)
         nc.vector.memset(up_planes_0[:].bitcast(I32), 0)
         nc.vector.memset(up_planes[:].bitcast(I32), 0)
         nc.vector.memset(down_planes[:].bitcast(I32), 0)
@@ -77,8 +77,8 @@ def tile_llama4textexperts_e_kernel(
                 ),
             )
 
-        def load_planes(planes, scales):
-            for quadrant in range(QUADRANTS):
+        def load_planes(planes, scales, first=0):
+            for quadrant in range(first, QUADRANTS):
                 nc.sync.dma_start(
                     out=planes[32 * quadrant : 32 * quadrant + 16, :].bitcast(I32),
                     in_=scales[:, 4 * quadrant : 4 * quadrant + 4, :].bitcast(I32),
@@ -91,16 +91,16 @@ def tile_llama4textexperts_e_kernel(
                     in_=scales[0, 4 * quadrant : 4 * quadrant + 4, :].bitcast(I32),
                 )
 
-        def load_packed_planes_aside(planes, scales):
-            for quadrant in range(QUADRANTS):
+        def load_packed_planes_aside(planes, scales, quadrants=QUADRANTS):
+            for quadrant in range(quadrants):
                 nc.gpsimd.dma_start(
                     out=planes[32 * quadrant : 32 * quadrant + 16, :].bitcast(F32),
                     in_=scales[:, 4 * quadrant : 4 * quadrant + 4, :].bitcast(F32),
                 )
 
-        def load_columns(words, given, chunk):
+        def load_columns(words, given, chunk, chunks=1):
             e, g = divmod(chunk, CHUNKS)
-            cols = slice(g * K_PASS, (g + 1) * K_PASS)
+            cols = slice(g * K_PASS, (g + chunks) * K_PASS)
             nc.sync.dma_start(
                 out=words[:, e, cols].bitcast(I32),
                 in_=given[e].rearrange("p n t -> p (n t)").bitcast(I32)[:, cols],
@@ -120,14 +120,16 @@ def tile_llama4textexperts_e_kernel(
             return e if round_ % 2 == 0 and e < EXPERTS else None
 
         load_packed_planes_aside(gate_planes[:], gate_w_scales)
-        load_packed_planes_aside(up_planes[:], up_w_scales)
+        load_packed_planes_aside(up_planes[:], up_w_scales, QUADRANTS - 1)
         load_x(0, 1)
         load_planes_of_expert_0(gate_planes_0, gate_w_scales)
-        load_columns(gate_words, gate_w_words, 0)
+        load_columns(gate_words, gate_w_words, 0, chunks=2)
         for round_ in range(N_ROUNDS + 2):
             for chunk in range(round_ * RUN, (round_ + 1) * RUN):
-                if chunk + 1 < N_CHUNKS:
+                if 1 < chunk + 1 < N_CHUNKS:
                     load_columns(gate_words, gate_w_words, chunk + 1)
+                if chunk == 2:
+                    load_planes(up_planes[:], up_w_scales, QUADRANTS - 1)
                 if chunk < N_CHUNKS:
                     load_columns(up_words, up_w_words, chunk)
                 if chunk == 0:
@@ -300,9 +302,12 @@ def tile_llama4textexperts_e_kernel(
                     ]
                     if first - 2 * RUN == N_CHUNKS - CHUNKS:
                         half = HIDDEN // 2
-                        pieces_of[1] = [
-                            (pieces_of[1][0][0][:, 0:half], slice(0, half)),
-                            (psum.tile([P, half], F32, tag="gate", name="sums_half"), slice(half, HIDDEN)),
+                        pieces_of = [
+                            [
+                                (pieces[0][0][:, 0:half], slice(0, half)),
+                                (psum.tile([P, half], F32, tag="gate", name="sums_half"), slice(half, HIDDEN)),
+                            ]
+                            for pieces in pieces_of
                         ]
                 for i in range(TOKEN_TILES):
                     add_to_out((first - 2 * RUN, second - 2 * RUN), i, pieces_of[i])

@@ -54,8 +54,8 @@ def tile_llama4textexperts_e_kernel(
         gate_planes = keep.tile([P, WIDE], U8, align_bytes=64)
         up_planes = keep.tile([P, WIDE], U8, align_bytes=64)
         down_planes = keep.tile([P, EXPERTS, HIDDEN], U8, align_bytes=64)
-        gate_planes_0 = keep.tile([P, WIDE], U8, align_bytes=64)
-        up_planes_0 = keep.tile([P, WIDE], U8, align_bytes=64)
+        gate_planes_0 = keep.tile([P, K_PASS], U8, align_bytes=64)
+        up_planes_0 = keep.tile([P, K_PASS], U8, align_bytes=64)
         out_sb = keep.tile([P, EXPERTS, TOKEN_TILES, HIDDEN], F32)
         identity = keep.tile([P, P], F32)
 
@@ -87,8 +87,10 @@ def tile_llama4textexperts_e_kernel(
         def load_planes_of_expert_0(planes, scales):
             for quadrant in range(QUADRANTS):
                 nc.sync.dma_start(
-                    out=planes[32 * quadrant : 32 * quadrant + 4, :].bitcast(I32),
-                    in_=scales[0, 4 * quadrant : 4 * quadrant + 4, :].bitcast(I32),
+                    out=planes[32 * quadrant : 32 * quadrant + 16, :].bitcast(I32),
+                    in_=scales[0, 4 * quadrant : 4 * quadrant + 4, :]
+                    .bitcast(I32)
+                    .rearrange("r (g n) -> g r n", g=CHUNKS),
                 )
 
         def load_packed_planes_aside(planes, scales, quadrants=QUADRANTS):
@@ -201,7 +203,7 @@ def tile_llama4textexperts_e_kernel(
                 lhsT=x_codes[:, e, tokens].bitcast(FP8X4),
                 lhsT_scale=x_scales[:, e, tokens],
                 rhs=words[:, e, cols].bitcast(FP8X4),
-                rhs_scale=planes_0[:, cols] if e == 0 else planes[4 * e : P, cols],
+                rhs_scale=planes_0[4 * g : P, :] if e == 0 else planes[4 * e : P, cols],
                 start=True,
                 stop=True,
             )

@@ -132,7 +132,9 @@ def tile_llama4textexperts_e_kernel(
                     load_columns(gate_words, gate_w_words, chunk + 1)
                 if chunk == 2:
                     load_planes(up_planes[:], up_w_scales, QUADRANTS - 1)
-                if chunk < N_CHUNKS:
+                if chunk == 0:
+                    load_columns(up_words, up_w_words, 0, chunks=2)
+                elif 1 < chunk < N_CHUNKS:
                     load_columns(up_words, up_w_words, chunk)
                 if chunk == 0:
                     load_planes_of_expert_0(up_planes_0, up_w_scales)
@@ -168,7 +170,18 @@ def tile_llama4textexperts_e_kernel(
             )
 
         def x_words(e, i, u):
+            if e in x_sorted:
+                return x_sorted[e][:, i, u, :]
             return x_sb[:, e, i, :].bitcast(F32)[:, u : HIDDEN // 2 : 2]
+
+        x_sorted = {}
+
+        def sort_x(e):
+            tile = work.tile([P, TOKEN_TILES, 2, P], F32, tag="x_sorted", name="x_sorted")
+            nc.scalar.copy(
+                out=tile[:], in_=x_sb[:, e].bitcast(F32).rearrange("p i (q u) -> p i u q", u=2)
+            )
+            x_sorted[e] = tile
 
         def transpose_x(e):
             def x_word_columns(i, u):
@@ -227,22 +240,24 @@ def tile_llama4textexperts_e_kernel(
                 op=MULT,
             )
 
+        def h_words(h, i, u):
+            return h[:, i, u].rearrange("p q j -> p (q j)").bitcast(F32)
+
         def transpose_h(h):
             def h_word_columns(i, u):
-                return h[:, i, u].rearrange("p q j -> p (q j)").bitcast(F32)
+                return h_words(h, i, u)
 
             return transpose_words(h_word_columns, "turned")
 
         def add_to_out(chunks, i, pieces):
-            tokens = slice(i * P, (i + 1) * P)
             for chunk in chunks:
                 e, g = divmod(chunk, CHUNKS)
-                codes, scales = quantised[chunk]
+                codes, scales = quantised[chunk, i]
                 for sums, cols in pieces:
                     nc.tensor.matmul_mx(
                         out=sums[:],
-                        lhsT=codes[:, tokens].bitcast(FP8X4),
-                        lhsT_scale=scales[:, tokens],
+                        lhsT=codes.bitcast(FP8X4),
+                        lhsT_scale=scales,
                         rhs=down_words[:, e, g, cols].bitcast(FP8X4),
                         rhs_scale=down_planes[4 * g : P, e, cols],
                         start=(g == 0),
@@ -274,10 +289,41 @@ def tile_llama4textexperts_e_kernel(
                 if 0 <= chunk < N_CHUNKS:
                     make_h(h_of[chunk], silu_of[chunk], chunk, i)
 
+        def turn_last(first):
+            turned = []
+            for i in range(TOKEN_TILES):
+                bank = psum.tile([P, RUN, 2, P], F32, tag="turned", name="turned_last")
+                for run in range(RUN):
+                    for u in range(2):
+                        nc.tensor.transpose(bank[:, run, u, :], h_words(h_of[first + run], i, u), identity[:])
+                turned.append(bank)
+            grouped = []
+            for bank, copy in zip(turned, (nc.scalar.copy, nc.vector.tensor_copy)):
+                tile = work.tile([P, RUN, P, PACK], BF16, tag="grouped", name="grouped_last", bufs=4, align_bytes=64)
+                copy(
+                    out=tile[:].rearrange("p c r t -> p (c r t)").bitcast(F32).rearrange(
+                        "p (c r u) -> p c r u", c=RUN, u=2
+                    ),
+                    in_=bank[:].rearrange("p c u r -> p c r u"),
+                )
+                grouped.append(tile)
+            for i in range(TOKEN_TILES):
+                codes = work.tile([P, RUN, P], U32, tag="h_codes", name="codes_last", bufs=4, align_bytes=64)
+                scales = work.tile([P, RUN, P], U8, tag="h_scales", name="scales_last", bufs=4, align_bytes=64)
+                nc.vector.quantize_mx(
+                    out=codes[:].rearrange("p c r -> p (c r)").bitcast(FP8X4),
+                    scales=scales[:].rearrange("p c r -> p (c r)"),
+                    in_=grouped[i][:].rearrange("p c r t -> p (c r t)"),
+                )
+                for run in range(RUN):
+                    quantised[first + run, i] = (codes[:, run, :], scales[:, run, :])
+
         make(-1)
         for round_ in range(N_ROUNDS + 2):
             first, second = round_ * RUN, round_ * RUN + 1
-            to_quantise = 1 <= round_ <= N_ROUNDS
+            to_quantise = 1 <= round_ < N_ROUNDS
+            if round_ == N_ROUNDS:
+                turn_last(first - RUN)
             make(first)
             next_expert = expert_turned_in(round_)
             if next_expert is not None:
@@ -295,7 +341,12 @@ def tile_llama4textexperts_e_kernel(
                     codes = work.tile([P, TOKENS], U32, tag="h_codes", bufs=4, align_bytes=64)
                     scales = work.tile([P, TOKENS], U8, tag="h_scales", bufs=4, align_bytes=64)
                     quantise(grouped, codes[:], scales[:])
-                    quantised[chunk] = (codes, scales)
+                    for i in range(TOKEN_TILES):
+                        tokens = slice(i * P, (i + 1) * P)
+                        quantised[chunk, i] = (codes[:, tokens], scales[:, tokens])
+            e_ahead = expert_turned_in(round_ + 1)
+            if e_ahead == 2:
+                sort_x(e_ahead)
             if round_ >= 2:
                 if (first - 2 * RUN) % CHUNKS == 0:
                     pieces_of = [

from contextlib import ExitStack

import concourse.mybir as mybir
from concourse.masks import make_identity

F32 = mybir.dt.float32
BF16 = mybir.dt.bfloat16
I32 = mybir.dt.int32
U32 = mybir.dt.uint32
U8 = mybir.dt.uint8
FP8X4 = mybir.dt.float8_e4m3fn_x4
SILU = mybir.ActivationFunctionType.Silu
MULT = mybir.AluOpType.mult

P = 128
PACK = 4
K_PASS = P * PACK
EXPERTS, TOKENS, HIDDEN, WIDE = 4, 256, 512, 2048
TOKEN_TILES = TOKENS // P
CHUNKS = WIDE // K_PASS
N_CHUNKS = EXPERTS * CHUNKS
QUADRANTS = 4
RUN = 2
N_ROUNDS = N_CHUNKS // RUN
GATE_BANKS = {1: "turned", 3: "sums"}

FLOPS = 3 * 2 * EXPERTS * TOKENS * HIDDEN * WIDE


def tile_llama4textexperts_e_kernel(
    tc,
    hidden_states,
    gate_w_words,
    gate_w_scales,
    up_w_words,
    up_w_scales,
    down_w_words,
    down_w_scales,
    out,
):
    nc = tc.nc
    with ExitStack() as stack:
        keep = stack.enter_context(tc.tile_pool(name="keep", bufs=1))
        work = stack.enter_context(tc.tile_pool(name="work", bufs=3))
        psum = stack.enter_context(tc.psum_pool(name="psum", bufs=2))
        stack.enter_context(tc.manual_schedule())

        x_sb = keep.tile([P, EXPERTS, TOKEN_TILES, HIDDEN], BF16)
        x_codes = keep.tile([P, EXPERTS, TOKENS], U32, align_bytes=64)
        x_scales = keep.tile([P, EXPERTS, TOKENS], U8, align_bytes=64)
        gate_words = keep.tile([P, EXPERTS, WIDE], U32, align_bytes=64)
        up_words = keep.tile([P, EXPERTS, WIDE], U32, align_bytes=64)
        down_words = keep.tile([P, EXPERTS, CHUNKS, HIDDEN], U32, align_bytes=64)
        gate_planes = keep.tile([P, WIDE], U8, align_bytes=64)
        up_planes = keep.tile([P, WIDE], U8, align_bytes=64)
        down_planes = keep.tile([P, EXPERTS, HIDDEN], U8, align_bytes=64)
        gate_planes_0 = keep.tile([P, K_PASS], U8, align_bytes=64)
        up_planes_0 = keep.tile([P, K_PASS], U8, align_bytes=64)
        out_sb = keep.tile([P, EXPERTS, TOKEN_TILES, HIDDEN], F32)
        identity = keep.tile([P, P], F32)

        warm = keep.tile([P, 2], F32)
        nc.vector.memset(gate_planes_0[:].bitcast(I32), 0)
        nc.vector.memset(gate_planes[:].bitcast(I32), 0)
        nc.vector.memset(warm[:, 0:1], 0.0)
        nc.scalar.activation(out=warm[:, 1:2], in_=warm[:, 0:1], func=SILU)
        nc.vector.memset(up_planes_0[:].bitcast(I32), 0)
        nc.vector.memset(up_planes[:].bitcast(I32), 0)
        nc.vector.memset(down_planes[:].bitcast(I32), 0)
        make_identity(nc, identity[:])

        def load_x(first, last):
            nc.sync.dma_start(
                out=x_sb[:, first:last].rearrange("p e i k -> p e (i k)"),
                in_=hidden_states[first * TOKENS : last * TOKENS, :].rearrange(
                    "(e p i) k -> p e (i k)", p=P, i=TOKEN_TILES
                ),
            )

        def load_planes(planes, scales, first=0):
            for quadrant in range(first, QUADRANTS):
                nc.sync.dma_start(
                    out=planes[32 * quadrant : 32 * quadrant + 16, :].bitcast(I32),
                    in_=scales[:, 4 * quadrant : 4 * quadrant + 4, :].bitcast(I32),
                )

        def load_planes_of_expert_0(planes, scales):
            for quadrant in range(QUADRANTS):
                nc.sync.dma_start(
                    out=planes[32 * quadrant : 32 * quadrant + 16, :].bitcast(I32),
                    in_=scales[0, 4 * quadrant : 4 * quadrant + 4, :]
                    .bitcast(I32)
                    .rearrange("r (g n) -> g r n", g=CHUNKS),
                )

        def load_packed_planes_aside(planes, scales, quadrants=QUADRANTS):
            for quadrant in range(quadrants):
                nc.gpsimd.dma_start(
                    out=planes[32 * quadrant : 32 * quadrant + 16, :].bitcast(F32),
                    in_=scales[:, 4 * quadrant : 4 * quadrant + 4, :].bitcast(F32),
                )

        def load_columns(words, given, chunk, chunks=1):
            e, g = divmod(chunk, CHUNKS)
            cols = slice(g * K_PASS, (g + chunks) * K_PASS)
            nc.sync.dma_start(
                out=words[:, e, cols].bitcast(I32),
                in_=given[e].rearrange("p n t -> p (n t)").bitcast(I32)[:, cols],
            )

        def load_rows(chunk):
            e, g = divmod(chunk, CHUNKS)
            if g == 0:
                load_planes(down_planes[:, e, :], down_w_scales[e * CHUNKS : (e + 1) * CHUNKS])
            nc.sync.dma_start(
                out=down_words[:, e, g, :].bitcast(I32),
                in_=down_w_words[chunk].rearrange("p n t -> p (n t)").bitcast(I32),
            )

        def expert_turned_in(round_):
            e = round_ // 2 + 1
            return e if round_ % 2 == 0 and e < EXPERTS else None

        load_packed_planes_aside(gate_planes[:], gate_w_scales)
        load_packed_planes_aside(up_planes[:], up_w_scales, QUADRANTS - 1)
        load_x(0, 1)
        load_planes_of_expert_0(gate_planes_0, gate_w_scales)
        load_columns(gate_words, gate_w_words, 0, chunks=2)
        for round_ in range(N_ROUNDS + 2):
            for chunk in range(round_ * RUN, (round_ + 1) * RUN):
                if 1 < chunk + 1 < N_CHUNKS:
                    load_columns(gate_words, gate_w_words, chunk + 1)
                if chunk == 2:
                    load_planes(up_planes[:], up_w_scales, QUADRANTS - 1)
                if chunk == 0:
                    load_columns(up_words, up_w_words, 0, chunks=2)
                elif 1 < chunk < N_CHUNKS:
                    load_columns(up_words, up_w_words, chunk)
                if chunk == 0:
                    load_planes_of_expert_0(up_planes_0, up_w_scales)
                if chunk == round_ * RUN and expert_turned_in(round_) is not None:
                    load_x(expert_turned_in(round_), expert_turned_in(round_) + 1)
            for chunk in range((round_ - 2) * RUN, (round_ - 1) * RUN):
                if chunk >= 0:
                    load_rows(chunk)

        def transpose_words(word_columns, tag):
            turned = psum.tile([P, TOKEN_TILES, 2, P], F32, tag=tag)
            for i in range(TOKEN_TILES):
                for u in range(2):
                    nc.tensor.transpose(turned[:, i, u, :], word_columns(i, u), identity[:])
            return turned

        def regroup(turned, copy):
            grouped = work.tile([P, TOKENS, PACK], BF16, tag="grouped", bufs=4, align_bytes=64)
            pairs = (
                grouped[:]
                .rearrange("p r t -> p (r t)")
                .bitcast(F32)
                .rearrange("p (i r u) -> p i r u", i=TOKEN_TILES, u=2)
            )
            copy(out=pairs, in_=turned[:].rearrange("p i u r -> p i r u"))
            return grouped

        def quantise(grouped, codes, scales):
            nc.vector.quantize_mx(
                out=codes.bitcast(FP8X4),
                scales=scales,
                in_=grouped[:].rearrange("p r t -> p (r t)"),
            )

        def x_words(e, i, u):
            if e in x_sorted:
                return x_sorted[e][:, i, u, :]
            return x_sb[:, e, i, :].bitcast(F32)[:, u : HIDDEN // 2 : 2]

        x_sorted = {}

        def sort_x(e):
            tile = work.tile([P, TOKEN_TILES, 2, P], F32, tag="x_sorted", name="x_sorted")
            nc.scalar.copy(
                out=tile[:], in_=x_sb[:, e].bitcast(F32).rearrange("p i (q u) -> p i u q", u=2)
            )
            x_sorted[e] = tile

        def transpose_x(e):
            def x_word_columns(i, u):
                return x_words(e, i, u)

            return regroup(transpose_words(x_word_columns, "sums"), nc.scalar.copy)

        def quantise_x(e, grouped):
            quantise(grouped, x_codes[:, e, :], x_scales[:, e, :])

        x0_grouped = []
        for i in range(TOKEN_TILES):
            x0_turned = psum.tile([P, 2, P], F32, tag="sums")
            for u in range(2):
                nc.tensor.transpose(x0_turned[:, u, :], x_words(0, i, u), identity[:])
            x0_tile = work.tile([P, P, PACK], BF16, tag="grouped", bufs=4, align_bytes=64)
            nc.scalar.copy(
                out=x0_tile[:].rearrange("p r t -> p (r t)").bitcast(F32).rearrange("p (r u) -> p r u", u=2),
                in_=x0_turned[:].rearrange("p u r -> p r u"),
            )
            x0_grouped.append(x0_tile)
        for i in range(TOKEN_TILES):
            tokens = slice(i * P, (i + 1) * P)
            quantise(x0_grouped[i], x_codes[:, 0, tokens], x_scales[:, 0, tokens])

        def first_layer(product, words, planes_0, planes, chunk, i):
            e, g = divmod(chunk, CHUNKS)
            cols = slice(g * K_PASS, (g + 1) * K_PASS)
            tokens = slice(i * P, (i + 1) * P)
            nc.tensor.matmul_mx(
                out=product[:],
                lhsT=x_codes[:, e, tokens].bitcast(FP8X4),
                lhsT_scale=x_scales[:, e, tokens],
                rhs=words[:, e, cols].bitcast(FP8X4),
                rhs_scale=planes_0[4 * g : P, :] if e == 0 else planes[4 * e : P, cols],
                start=True,
                stop=True,
            )

        def make_silu(silu, chunk, i):
            gate_ps = psum.tile([P, K_PASS], F32, tag=GATE_BANKS.get(chunk, "gate"), name="gate_ps")
            first_layer(gate_ps, gate_words, gate_planes_0, gate_planes, chunk, i)
            nc.scalar.activation(
                out=silu[:, i],
                in_=gate_ps[:].rearrange("p (q u j) -> p u q j", u=2, j=2),
                func=SILU,
            )

        def make_h(h, silu, chunk, i):
            up_ps = psum.tile([P, K_PASS], F32, tag="up")
            first_layer(up_ps, up_words, up_planes_0, up_planes, chunk, i)
            nc.vector.tensor_tensor(
                out=h[:, i],
                in0=up_ps[:].rearrange("p (q u j) -> p u q j", u=2, j=2),
                in1=silu[:, i],
                op=MULT,
            )

        def h_words(h, i, u):
            return h[:, i, u].rearrange("p q j -> p (q j)").bitcast(F32)

        def transpose_h(h):
            def h_word_columns(i, u):
                return h_words(h, i, u)

            return transpose_words(h_word_columns, "turned")

        def add_to_out(chunks, i, pieces):
            for chunk in chunks:
                e, g = divmod(chunk, CHUNKS)
                codes, scales = quantised[chunk, i]
                for sums, cols in pieces:
                    nc.tensor.matmul_mx(
                        out=sums[:],
                        lhsT=codes.bitcast(FP8X4),
                        lhsT_scale=scales,
                        rhs=down_words[:, e, g, cols].bitcast(FP8X4),
                        rhs_scale=down_planes[4 * g : P, e, cols],
                        start=(g == 0),
                        stop=(g == CHUNKS - 1),
                    )
            if g == CHUNKS - 1:
                rows = out[e * TOKENS : (e + 1) * TOKENS, :].rearrange(
                    "(p i) n -> p i n", i=TOKEN_TILES
                )
                for sums, cols in pieces[:-1]:
                    nc.vector.tensor_copy(out=out_sb[:, e, i, cols], in_=sums[:])
                    nc.sync.dma_start(out=rows[:, i, cols], in_=out_sb[:, e, i, cols])
                sums, cols = pieces[-1]
                nc.scalar.copy(out=out_sb[:, e, i, cols], in_=sums[:])
                nc.sync.dma_start(out=rows[:, i, cols], in_=out_sb[:, e, i, cols])

        silu_of = {}
        h_of = {}
        quantised = {}

        def make(chunk):
            if chunk + 1 < N_CHUNKS:
                silu_of[chunk + 1] = work.tile([P, TOKEN_TILES, 2, P, 2], F32, tag="silu", name="silu")
            if 0 <= chunk < N_CHUNKS:
                h_of[chunk] = work.tile([P, TOKEN_TILES, 2, P, 2], BF16, tag="h", name="h")
            for i in range(TOKEN_TILES):
                if chunk + 1 < N_CHUNKS:
                    make_silu(silu_of[chunk + 1], chunk + 1, i)
                if 0 <= chunk < N_CHUNKS:
                    make_h(h_of[chunk], silu_of[chunk], chunk, i)

        def turn_last(first):
            turned = []
            for i in range(TOKEN_TILES):
                bank = psum.tile([P, RUN, 2, P], F32, tag="turned", name="turned_last")
                for run in range(RUN):
                    for u in range(2):
                        nc.tensor.transpose(bank[:, run, u, :], h_words(h_of[first + run], i, u), identity[:])
                turned.append(bank)
            grouped = []
            for bank, copy in zip(turned, (nc.scalar.copy, nc.vector.tensor_copy)):
                tile = work.tile([P, RUN, P, PACK], BF16, tag="grouped", name="grouped_last", bufs=4, align_bytes=64)
                copy(
                    out=tile[:].rearrange("p c r t -> p (c r t)").bitcast(F32).rearrange(
                        "p (c r u) -> p c r u", c=RUN, u=2
                    ),
                    in_=bank[:].rearrange("p c u r -> p c r u"),
                )
                grouped.append(tile)
            for i in range(TOKEN_TILES):
                codes = work.tile([P, RUN, P], U32, tag="h_codes", name="codes_last", bufs=4, align_bytes=64)
                scales = work.tile([P, RUN, P], U8, tag="h_scales", name="scales_last", bufs=4, align_bytes=64)
                nc.vector.quantize_mx(
                    out=codes[:].rearrange("p c r -> p (c r)").bitcast(FP8X4),
                    scales=scales[:].rearrange("p c r -> p (c r)"),
                    in_=grouped[i][:].rearrange("p c r t -> p (c r t)"),
                )
                for run in range(RUN):
                    quantised[first + run, i] = (codes[:, run, :], scales[:, run, :])

        make(-1)
        for round_ in range(N_ROUNDS + 2):
            first, second = round_ * RUN, round_ * RUN + 1
            to_quantise = 1 <= round_ < N_ROUNDS
            if round_ == N_ROUNDS:
                turn_last(first - RUN)
            make(first)
            next_expert = expert_turned_in(round_)
            if next_expert is not None:
                x_grouped = transpose_x(next_expert)
            if to_quantise:
                turned_first = transpose_h(h_of[first - RUN])
                turned_second = transpose_h(h_of[second - RUN])
                grouped_first = regroup(turned_first, nc.scalar.copy)
                grouped_second = regroup(turned_second, nc.vector.tensor_copy)
            make(second)
            if next_expert is not None:
                quantise_x(next_expert, x_grouped)
            if to_quantise:
                for chunk, grouped in ((first - RUN, grouped_first), (second - RUN, grouped_second)):
                    codes = work.tile([P, TOKENS], U32, tag="h_codes", bufs=4, align_bytes=64)
                    scales = work.tile([P, TOKENS], U8, tag="h_scales", bufs=4, align_bytes=64)
                    quantise(grouped, codes[:], scales[:])
                    for i in range(TOKEN_TILES):
                        tokens = slice(i * P, (i + 1) * P)
                        quantised[chunk, i] = (codes[:, tokens], scales[:, tokens])
            e_ahead = expert_turned_in(round_ + 1)
            if e_ahead == 2:
                sort_x(e_ahead)
            if round_ >= 2:
                if (first - 2 * RUN) % CHUNKS == 0:
                    pieces_of = [
                        [(psum.tile([P, HIDDEN], F32, tag="sums", name="sums%d" % i), slice(0, HIDDEN))]
                        for i in range(TOKEN_TILES)
                    ]
                    if first - 2 * RUN == N_CHUNKS - CHUNKS:
                        half = HIDDEN // 2
                        pieces_of = [
                            [
                                (pieces[0][0][:, 0:half], slice(0, half)),
                                (psum.tile([P, half], F32, tag="gate", name="sums_half"), slice(half, HIDDEN)),
                            ]
                            for pieces in pieces_of
                        ]
                for i in range(TOKEN_TILES):
                    add_to_out((first - 2 * RUN, second - 2 * RUN), i, pieces_of[i])
